import numpy as np
import ml_dtypes


def mxq(x, axis, fmt="e4m3"):
    dtype, down = {"e4m3": (ml_dtypes.float8_e4m3fn, 7), "e5m2": (ml_dtypes.float8_e5m2, 14)}[fmt]
    v = np.moveaxis(np.asarray(x, np.float32).astype(ml_dtypes.bfloat16).astype(np.float64), axis, -1)
    blocks = v.reshape(v.shape[:-1] + (-1, 32))
    amax = np.abs(blocks).max(-1, keepdims=True)
    byte = np.maximum(np.where(amax > 0, np.frexp(amax)[1] - 1 + 127, 0) - down, 1)
    scale = np.exp2(byte - 127.0)
    codes = (blocks / scale).astype(np.float32).astype(dtype).astype(np.float64)
    return np.moveaxis((codes * scale).reshape(v.shape), -1, axis)


WIDE = False


def mx_kscale(k):
    if not WIDE:
        return np.ones(k)
    levels = np.array([10, -10, 5, -5, 0])
    a = np.random.permutation(np.resize(levels, k // 512 * 4)).reshape(k // 512, 4)
    idx = np.arange(k)
    return np.exp2(a[idx // 512, idx % 128 // 32])


BF16 = ml_dtypes.bfloat16


def bf(x):
    return np.asarray(x, np.float32).astype(BF16)


def f64(x):
    return np.asarray(x).astype(np.float64)


B, C, P, NH, NW = 4, 4, 16, 16, 16
D = C * P * P
QK_SCALE = 1.0


def rel_bias(p):
    i = np.arange(p, dtype=np.float64)
    down = np.exp(-i / (p / 2))[:, None] * np.ones((1, p))
    right = down.T
    br = np.exp(-(i[:, None] + i[None, :]) / (p / 2))
    return np.stack([
        np.rot90(br, 2), np.flip(down, 0), np.rot90(br, 1),
        np.flip(right, 1), np.ones((p, p)), right,
        np.rot90(br, 3), down, br,
    ], axis=0)


def setup_inputs():
    s = mx_kscale(D)
    sx = np.tile(s.reshape(C, P, P), (1, NH, NW))
    return {"x": bf(np.random.standard_normal((B, C, NH * P, NW * P)) * sx),
            "W_qkv": bf(np.random.standard_normal((3 * D, D)) / np.sqrt(D) / s),
            "b_qkv": bf(np.random.standard_normal(3 * D) * 0.5)}


def reference(x, W_qkv, b_qkv):
    p, c = P, C
    b, _, h, w = x.shape
    nh, nw = h // p, w // p
    feat = f64(x).reshape(b, c, nh, p, nw, p).transpose(0, 2, 4, 1, 3, 5).reshape(b, nh, nw, c * p * p)
    y = mxq(feat, 3, "e4m3") @ mxq(f64(W_qkv), 1, "e4m3").T
    qkv = np.pad(y, ((0, 0), (1, 1), (1, 1), (0, 0))) + f64(b_qkv)
    qkv = qkv.reshape(b, nh + 2, nw + 2, 3, c, p, p)
    core_q = qkv[:, 1:nh + 1, 1:nw + 1, 0] * QK_SCALE
    k = np.stack([qkv[:, di:di + nh, dj:dj + nw, 1] for di in range(3) for dj in range(3)], axis=3)
    v = np.stack([qkv[:, di:di + nh, dj:dj + nw, 2] for di in range(3) for dj in range(3)], axis=3)
    bias = rel_bias(p)
    attn = core_q[:, :, :, None] * k * bias[:, None]
    out = np.sum(attn * v, axis=3)
    return out.transpose(0, 3, 1, 4, 2, 5).reshape(b, c, nh * p, nw * p)

@@ -1,0 +1,303 @@
+from contextlib import ExitStack
+
+import concourse.mybir as mybir
+from concourse.masks import make_identity
+
+F32 = mybir.dt.float32
+BF16 = mybir.dt.bfloat16
+U32 = mybir.dt.uint32
+U8 = mybir.dt.uint8
+I32 = mybir.dt.int32
+FP8X4 = mybir.dt.float8_e4m3fn_x4
+ALU = mybir.AluOpType
+ACT = mybir.ActivationFunctionType
+
+FLOPS = 2 * 1024 * 1024 * 3072
+
+P = 128
+NCHUNK = 8
+NHALF = 2
+COLS = 512
+YB = 32
+TROW = 48
+
+
+def tile_attentionconv_kernel(tc, x, W_qkv, b_qkv, out):
+    nc = tc.nc
+    with ExitStack() as ctx:
+        const = ctx.enter_context(tc.tile_pool(name="const", bufs=1))
+        xpool = ctx.enter_context(tc.tile_pool(name="xpool", bufs=1))
+        wnat = ctx.enter_context(tc.tile_pool(name="wnat", bufs=NCHUNK))
+        wgrp = ctx.enter_context(tc.tile_pool(name="wgrp", bufs=2))
+        wq = ctx.enter_context(tc.tile_pool(name="wq", bufs=3))
+        work = ctx.enter_context(tc.tile_pool(name="work", bufs=2))
+        outp = ctx.enter_context(tc.tile_pool(name="outp", bufs=2))
+        ps_mx = ctx.enter_context(tc.psum_pool(name="ps_mx", bufs=2))
+        ps_tp = ctx.enter_context(tc.psum_pool(name="ps_tp", bufs=2))
+
+        b_rows = const.tile([P, P], BF16, name="b_rows")
+        nc.vector.memset(b_rows[:], 0.0)
+        nc.scalar.dma_start(out=b_rows[0:24, :], in_=b_qkv.rearrange("(t p) -> t p", p=P))
+
+        xn = []
+        wn = []
+
+        def load_x(h):
+            t = xpool.tile([P, 4096], BF16, name="xn%d" % h)
+            for ch in range(4):
+                for bl in range(2):
+                    base = ch * 32 + bl
+                    nc.sync.dma_start(
+                        out=t[base : base + 31 : 2, :],
+                        in_=x[2 * h + bl, ch].rearrange("(i r) w -> i (r w)", r=16),
+                    )
+            xn.append(t)
+
+        w_view = W_qkv.rearrange("(s c p) k -> c p s k", s=3, c=NCHUNK, p=P)
+
+        def load_w(c):
+            t = wnat.tile([P, 3, 1024], BF16, name="wn", tag="wn")
+            nc.sync.dma_start(out=t[:], in_=w_view[c])
+            wn.append(t)
+
+        load_x(0)
+        load_w(0)
+        load_x(1)
+        for c in range(1, NCHUNK):
+            load_w(c)
+
+        ident = const.tile([P, P], F32, name="ident")
+        make_identity(nc, ident[:])
+        ones = const.tile([P, P], F32, name="ones")
+        nc.gpsimd.memset(ones[:], 1.0)
+        pidx = const.tile([P, 1], I32, name="pidx")
+        nc.gpsimd.iota(pidx[:], pattern=[[0, 1]], base=0, channel_multiplier=1)
+        s_i = const.tile([P, 1], I32, name="s_i")
+        nc.vector.tensor_single_scalar(out=s_i[:], in_=pidx[:], scalar=15, op=ALU.bitwise_and)
+        r_i = const.tile([P, 1], I32, name="r_i")
+        nc.vector.tensor_single_scalar(out=r_i[:], in_=pidx[:], scalar=4, op=ALU.logical_shift_right)
+        s_f = const.tile([P, 1], F32, name="s_f")
+        nc.vector.tensor_copy(out=s_f[:], in_=s_i[:])
+        r_f = const.tile([P, 1], F32, name="r_f")
+        nc.vector.tensor_copy(out=r_f[:], in_=r_i[:])
+        tab = const.tile([P, 8], F32, name="tab")
+        nc.scalar.activation(out=tab[:, 0:1], in_=s_f[:], func=ACT.Exp, scale=0.125, bias=-1.875)
+        nc.scalar.activation(out=tab[:, 1:2], in_=s_f[:], func=ACT.Exp, scale=-0.125)
+        for rh in range(2):
+            nc.scalar.activation(
+                out=tab[:, 2 + rh : 3 + rh], in_=r_f[:], func=ACT.Exp, scale=0.125, bias=(8.0 * rh - 15.0) / 8.0
+            )
+            nc.scalar.activation(
+                out=tab[:, 4 + rh : 5 + rh], in_=r_f[:], func=ACT.Exp, scale=-0.125, bias=-1.0 * rh
+            )
+        hs = const.tile([P, 1], F32, name="hs")
+        nc.vector.scalar_tensor_tensor(
+            out=hs[:], in0=tab[:, 0:1], scalar=1.0, in1=tab[:, 1:2], op0=ALU.add, op1=ALU.add
+        )
+
+        b_rows_f = const.tile([P, P], F32, name="b_rows_f")
+        nc.vector.tensor_copy(out=b_rows_f[:], in_=b_rows[:])
+        b_ps = ps_tp.tile([P, 4, P], F32, name="b_ps", tag="tp")
+        nc.tensor.transpose(out=b_ps[:, 0, :], in_=b_rows_f[:], identity=ident[:])
+        bias = const.tile([P, 24], F32, name="bias")
+        nc.vector.tensor_copy(out=bias[:], in_=b_ps[:, 0, 0:24])
+        cb = const.tile([P, NCHUNK], F32, name="cb")
+        nc.vector.tensor_mul(out=cb[:], in0=bias[:, 8:16], in1=bias[:, 16:24])
+        cbh = const.tile([P, NCHUNK], F32, name="cbh")
+        nc.vector.tensor_scalar_mul(out=cbh[:], in0=cb[:], scalar1=hs[:, 0:1])
+
+        xc = {}
+        xs = {}
+
+        def x_prep(h):
+            src = xn[h][:].bitcast(F32).rearrange("p (r j s) -> p j r s", r=16, j=16, s=8)
+            xr = xpool.tile([P, 2048], F32, name="xr%d" % h)
+            xr_v = xr[:].rearrange("p (j r s) -> p j r s", j=16, r=16, s=8)
+            xg = [xpool.tile([P, 2048], BF16, name="xg%d_%d" % (h, g), align_bytes=64) for g in range(2)]
+            for q in range(4):
+                js = slice(4 * q, 4 * q + 4)
+                if q == 1:
+                    nc.scalar.copy(out=xr_v[:, js], in_=src[:, js])
+                else:
+                    nc.vector.tensor_copy(out=xr_v[:, js], in_=src[:, js])
+            for q in range(4):
+                xt = ps_tp.tile([P, 4, P], F32, name="xt", tag="tp")
+                for jj in range(4):
+                    j = 4 * q + jj
+                    nc.tensor.transpose(out=xt[:, jj, :], in_=xr[:, j * P : (j + 1) * P], identity=ident[:])
+                xt_v = xt[:].rearrange("p j (c y) -> p j c y", c=4)
+                for g in range(2):
+                    dst = xg[g][:].bitcast(F32).rearrange("p (j y u) -> p j y u", j=16, y=YB, u=2)[:, 4 * q : 4 * q + 4]
+                    piece = xt_v[:, :, 2 * g : 2 * g + 2, :].rearrange("p j u y -> p j y u")
+                    if q % 2 == 0:
+                        nc.vector.tensor_copy(out=dst, in_=piece)
+                    else:
+                        nc.scalar.copy(out=dst, in_=piece)
+            for g in range(2):
+                codes = xpool.tile([P, COLS], U32, name="xc%d_%d" % (h, g), align_bytes=64)
+                scales = xpool.tile([P, COLS], U8, name="xs%d_%d" % (h, g), align_bytes=64)
+                nc.vector.quantize_mx(out=codes[:].bitcast(FP8X4), scales=scales[:], in_=xg[g][:])
+                xc[(h, g)] = codes
+                xs[(h, g)] = scales
+
+        wc = {}
+        ws = {}
+        SECTION = (1, 2, 0)
+
+        def w_prep(c):
+            wg = wgrp.tile([P, 3072], BF16, name="wg", tag="wg", align_bytes=64)
+            wg_v = wg[:].bitcast(F32).rearrange("p (t g o u) -> p t g o u", t=3, g=2, o=P, u=2)
+            for t in range(3):
+                wt = ps_tp.tile([P, 4, P], F32, name="wt", tag="tp")
+                words = wn[c][:, SECTION[t], :].bitcast(F32)
+                for chn in range(4):
+                    nc.tensor.transpose(out=wt[:, chn, :], in_=words[:, chn * P : (chn + 1) * P], identity=ident[:])
+                nc.scalar.copy(out=wg_v[:, t], in_=wt[:].rearrange("p (g u) o -> p g o u", g=2, u=2))
+            codes = wq.tile([P, 768], U32, name="wc", tag="wc", align_bytes=64)
+            scales = wq.tile([P, 768], U8, name="ws", tag="ws", align_bytes=64)
+            nc.vector.quantize_mx(out=codes[:, 0:512].bitcast(FP8X4), scales=scales[:, 0:512], in_=wg[:, 0:2048])
+            nc.vector.quantize_mx(out=codes[:, 512:768].bitcast(FP8X4), scales=scales[:, 512:768], in_=wg[:, 2048:3072])
+            wc[c] = codes
+            ws[c] = scales
+
+        def mx(c, h, t):
+            acc = ps_mx.tile([P, COLS], F32, name="acc", tag="acc%d" % t)
+            for g in range(2):
+                cols = slice(t * 256 + g * P, t * 256 + (g + 1) * P)
+                nc.tensor.matmul_mx(
+                    out=acc[:],
+                    lhsT=wc[c][:, cols].bitcast(FP8X4),
+                    lhsT_scale=ws[c][:, cols],
+                    rhs=xc[(h, g)][:].bitcast(FP8X4),
+                    rhs_scale=xs[(h, g)][:],
+                    start=(g == 0),
+                    stop=(g == 1),
+                )
+            return acc
+
+        k_sb = {}
+        v_ps = {}
+        kv = {}
+        tt = {}
+
+        def front(c, h):
+            k_ps = mx(c, h, 0)
+            v_ps[(c, h)] = mx(c, h, 1)
+            ks = work.tile([P, COLS], F32, name="ks", tag="ks%d" % h)
+            nc.scalar.activation(out=ks[:], in_=k_ps[:], func=ACT.Identity, bias=bias[:, 8 + c : 9 + c], scale=1.0)
+            k_sb[(c, h)] = ks
+            kvt = work.tile([P, 18, YB], F32, name="kvt", tag="kv%d" % h)
+            nc.scalar.activation(
+                out=kvt[:, 0:18:17, :],
+                in_=ones[:, 0:64].rearrange("p (a y) -> p a y", a=2),
+                func=ACT.Copy,
+                scale=cb[:, c : c + 1],
+            )
+            kv[(c, h)] = kvt
+            ttt = work.tile([P, 16, TROW], F32, name="ttt", tag="tt%d" % h)
+            nc.scalar.activation(
+                out=ttt[:].rearrange("p j (l f) -> p j l f", f=4)[:, :, 1:11:9, :],
+                in_=ones[:].rearrange("p (j l f) -> p j l f", j=16, l=2, f=4),
+                func=ACT.Copy,
+                scale=cbh[:, c : c + 1],
+            )
+            tt[(c, h)] = ttt
+
+        o_tiles = {}
+
+        def chunk(c):
+            ch = c // 2
+            rh = c % 2
+            halves = range(NHALF)
+            for h in halves:
+                flat = kv[(c, h)][:].rearrange("p a y -> p (a y)")
+                nc.vector.scalar_tensor_tensor(
+                    out=flat[:, YB : YB + COLS],
+                    in0=v_ps[(c, h)][:],
+                    scalar=bias[:, 16 + c : 17 + c],
+                    in1=k_sb[(c, h)][:],
+                    op0=ALU.add,
+                    op1=ALU.mult,
+                )
+            q_ps = [mx(c, h, 2) for h in halves]
+            if c + 1 < NCHUNK:
+                for h in halves:
+                    front(c + 1, h)
+            pp = []
+            for h in halves:
+                flat = kv[(c, h)][:].rearrange("p a y -> p (a y)")
+                pt = work.tile([P, COLS], F32, name="pt", tag="pt%d" % h)
+                nc.vector.scalar_tensor_tensor(
+                    out=pt[:], in0=flat[:, 0:COLS], scalar=tab[:, 0:1], in1=flat[:, YB : YB + COLS],
+                    op0=ALU.mult, op1=ALU.add,
+                )
+                pp.append(pt)
+            for h in halves:
+                nc.vector.scalar_tensor_tensor(
+                    out=tt[(c, h)][:, :, 8:40],
+                    in0=kv[(c, h)][:, 2:18, :],
+                    scalar=tab[:, 1:2],
+                    in1=pp[h][:].rearrange("p (j y) -> p j y", y=YB),
+                    op0=ALU.mult, op1=ALU.add,
+                )
+            qq = []
+            for h in halves:
+                qt = work.tile([P, 16, YB], F32, name="qt", tag="qt%d" % h)
+                nc.vector.scalar_tensor_tensor(
+                    out=qt[:], in0=tt[(c, h)][:, :, 6:38], scalar=tab[:, 2 + rh : 3 + rh], in1=tt[(c, h)][:, :, 8:40],
+                    op0=ALU.mult, op1=ALU.add,
+                )
+                qq.append(qt)
+            uu = []
+            for h in halves:
+                ut = work.tile([P, 16, YB], F32, name="ut", tag="ut%d" % h)
+                nc.vector.scalar_tensor_tensor(
+                    out=ut[:], in0=tt[(c, h)][:, :, 10:42], scalar=tab[:, 4 + rh : 5 + rh], in1=qq[h][:],
+                    op0=ALU.mult, op1=ALU.add,
+                )
+                uu.append(ut)
+            if c + 2 < NCHUNK:
+                w_prep(c + 2)
+            if rh == 0:
+                o_tiles[ch] = outp.tile([P, 16, 2, NHALF, YB], F32, name="ot", tag="ot")
+            for h in halves:
+                nc.vector.scalar_tensor_tensor(
+                    out=o_tiles[ch][:, :, rh, h, :],
+                    in0=q_ps[h][:].rearrange("p (j y) -> p j y", y=YB),
+                    scalar=bias[:, c : c + 1],
+                    in1=uu[h][:],
+                    op0=ALU.add, op1=ALU.mult,
+                )
+            if rh == 1:
+                store(ch)
+
+        def store(ch):
+            o_flat = o_tiles[ch][:].rearrange("p j a h y -> p (j a h y)")
+            os_t = outp.tile([P, 8, 16, 16], F32, name="os_t", tag="os")
+            for q in range(4):
+                tp = ps_tp.tile([P, 4, P], F32, name="tp", tag="tp")
+                for jj in range(4):
+                    j = 4 * q + jj
+                    nc.tensor.transpose(out=tp[:, jj, :], in_=o_flat[:, j * P : (j + 1) * P], identity=ident[:])
+                nc.scalar.copy(
+                    out=os_t[:, :, 4 * q : 4 * q + 4, :],
+                    in_=tp[:].rearrange("p j (r s) -> p r j s", r=8, s=16),
+                )
+            os_flat = os_t[:].rearrange("p r j s -> p (r j s)")
+            for rh in range(2):
+                for h in range(NHALF):
+                    for bl in range(2):
+                        base = rh * 64 + h * 32 + bl
+                        nc.sync.dma_start(
+                            out=out[2 * h + bl, ch].rearrange("(i a r) w -> a i (r w)", a=2, r=8)[rh],
+                            in_=os_flat[base : base + 31 : 2, :],
+                        )
+
+        x_prep(0)
+        w_prep(0)
+        front(0, 0)
+        x_prep(1)
+        front(0, 1)
+        w_prep(1)
+        for c in range(NCHUNK):
+            chunk(c)

@@ -16,10 +16,10 @@ FLOPS = 2 * 1024 * 1024 * 3072
 
 P = 128
 NCHUNK = 8
-NHALF = 2
-COLS = 512
-YB = 32
-TROW = 48
+NPATCH = 1024
+BANK = 512
+YJ = 64
+TROW = 80
 
 
 def tile_attentionconv_kernel(tc, x, W_qkv, b_qkv, out):
@@ -29,57 +29,50 @@ def tile_attentionconv_kernel(tc, x, W_qkv, b_qkv, out):
         xpool = ctx.enter_context(tc.tile_pool(name="xpool", bufs=1))
         wnat = ctx.enter_context(tc.tile_pool(name="wnat", bufs=NCHUNK))
         wgrp = ctx.enter_context(tc.tile_pool(name="wgrp", bufs=2))
-        wq = ctx.enter_context(tc.tile_pool(name="wq", bufs=3))
-        work = ctx.enter_context(tc.tile_pool(name="work", bufs=2))
+        wq = ctx.enter_context(tc.tile_pool(name="wq", bufs=4))
+        work2 = ctx.enter_context(tc.tile_pool(name="work2", bufs=2))
+        work1 = ctx.enter_context(tc.tile_pool(name="work1", bufs=1))
         outp = ctx.enter_context(tc.tile_pool(name="outp", bufs=2))
         ps_mx = ctx.enter_context(tc.psum_pool(name="ps_mx", bufs=2))
         ps_tp = ctx.enter_context(tc.psum_pool(name="ps_tp", bufs=2))
 
-        b_rows = const.tile([P, P], BF16, name="b_rows")
-        nc.vector.memset(b_rows[:], 0.0)
-        nc.scalar.dma_start(out=b_rows[0:24, :], in_=b_qkv.rearrange("(t p) -> t p", p=P))
+        vcopy = nc.vector.tensor_copy
+        scopy = nc.scalar.copy
 
+        def bank(tag):
+            pool = ps_tp if tag == "tp" else ps_mx
+            return pool.tile([P, 4, P], F32, name="bk", tag=tag)
+
+        b_rows = const.tile([24, P], BF16, name="b_rows")
+        nc.sync.dma_start(out=b_rows[:], in_=b_qkv.rearrange("(t p) -> t p", p=P))
+
+        x_rows = x.rearrange("b c (i r) w -> (b c i) (r w)", r=16)
         xn = []
-        wn = []
-
-        def load_x(h):
+        for h in range(2):
             t = xpool.tile([P, 4096], BF16, name="xn%d" % h)
-            for ch in range(4):
-                for bl in range(2):
-                    base = ch * 32 + bl
-                    nc.sync.dma_start(
-                        out=t[base : base + 31 : 2, :],
-                        in_=x[2 * h + bl, ch].rearrange("(i r) w -> i (r w)", r=16),
-                    )
+            nc.sync.dma_start(out=t[:], in_=x_rows[h * P : (h + 1) * P, :])
             xn.append(t)
-
         w_view = W_qkv.rearrange("(s c p) k -> c p s k", s=3, c=NCHUNK, p=P)
-
-        def load_w(c):
+        wn = []
+        for c in range(NCHUNK):
             t = wnat.tile([P, 3, 1024], BF16, name="wn", tag="wn")
             nc.sync.dma_start(out=t[:], in_=w_view[c])
             wn.append(t)
 
-        load_x(0)
-        load_w(0)
-        load_x(1)
-        for c in range(1, NCHUNK):
-            load_w(c)
-
         ident = const.tile([P, P], F32, name="ident")
         make_identity(nc, ident[:])
-        ones = const.tile([P, P], F32, name="ones")
-        nc.gpsimd.memset(ones[:], 1.0)
         pidx = const.tile([P, 1], I32, name="pidx")
         nc.gpsimd.iota(pidx[:], pattern=[[0, 1]], base=0, channel_multiplier=1)
+        ones = const.tile([P, P], F32, name="ones")
+        nc.gpsimd.memset(ones[:], 1.0)
         s_i = const.tile([P, 1], I32, name="s_i")
         nc.vector.tensor_single_scalar(out=s_i[:], in_=pidx[:], scalar=15, op=ALU.bitwise_and)
         r_i = const.tile([P, 1], I32, name="r_i")
         nc.vector.tensor_single_scalar(out=r_i[:], in_=pidx[:], scalar=4, op=ALU.logical_shift_right)
         s_f = const.tile([P, 1], F32, name="s_f")
-        nc.vector.tensor_copy(out=s_f[:], in_=s_i[:])
+        vcopy(out=s_f[:], in_=s_i[:])
         r_f = const.tile([P, 1], F32, name="r_f")
-        nc.vector.tensor_copy(out=r_f[:], in_=r_i[:])
+        vcopy(out=r_f[:], in_=r_i[:])
         tab = const.tile([P, 8], F32, name="tab")
         nc.scalar.activation(out=tab[:, 0:1], in_=s_f[:], func=ACT.Exp, scale=0.125, bias=-1.875)
         nc.scalar.activation(out=tab[:, 1:2], in_=s_f[:], func=ACT.Exp, scale=-0.125)
@@ -90,214 +83,285 @@ def tile_attentionconv_kernel(tc, x, W_qkv, b_qkv, out):
             nc.scalar.activation(
                 out=tab[:, 4 + rh : 5 + rh], in_=r_f[:], func=ACT.Exp, scale=-0.125, bias=-1.0 * rh
             )
+        perm = const.tile([P, P], F32, name="perm")
+        id_v = ident[:].rearrange("p (bl g u i) -> p g i bl u", bl=2, g=2, u=2, i=16)
+        pm_v = perm[:].rearrange("p (g i bl u) -> p g i bl u", g=2, i=16, bl=2, u=2)
+        for g in range(2):
+            vcopy(out=pm_v[:, g], in_=id_v[:, g])
         hs = const.tile([P, 1], F32, name="hs")
         nc.vector.scalar_tensor_tensor(
             out=hs[:], in0=tab[:, 0:1], scalar=1.0, in1=tab[:, 1:2], op0=ALU.add, op1=ALU.add
         )
-
         b_rows_f = const.tile([P, P], F32, name="b_rows_f")
-        nc.vector.tensor_copy(out=b_rows_f[:], in_=b_rows[:])
-        b_ps = ps_tp.tile([P, 4, P], F32, name="b_ps", tag="tp")
-        nc.tensor.transpose(out=b_ps[:, 0, :], in_=b_rows_f[:], identity=ident[:])
+        nc.vector.memset(b_rows_f[:], 0.0)
         bias = const.tile([P, 24], F32, name="bias")
-        nc.vector.tensor_copy(out=bias[:], in_=b_ps[:, 0, 0:24])
         cb = const.tile([P, NCHUNK], F32, name="cb")
-        nc.vector.tensor_mul(out=cb[:], in0=bias[:, 8:16], in1=bias[:, 16:24])
         cbh = const.tile([P, NCHUNK], F32, name="cbh")
-        nc.vector.tensor_scalar_mul(out=cbh[:], in0=cb[:], scalar1=hs[:, 0:1])
 
-        xc = {}
-        xs = {}
+        def bias_columns():
+            vcopy(out=b_rows_f[0:24, :], in_=b_rows[:])
+            b_ps = bank("tp")
+            nc.tensor.transpose(out=b_ps[:, 0, :], in_=b_rows_f[:], identity=ident[:])
+            vcopy(out=bias[:], in_=b_ps[:, 0, 0:24])
+            nc.vector.tensor_mul(out=cb[:], in0=bias[:, 8:16], in1=bias[:, 16:24])
+            nc.vector.tensor_scalar_mul(out=cbh[:], in0=cb[:], scalar1=hs[:, 0:1])
 
-        def x_prep(h):
+        xr = [xpool.tile([P, 2048], F32, name="xr%d" % h) for h in range(2)]
+        xg = [xpool.tile([P, 4096], BF16, name="xg%d" % g, align_bytes=64) for g in range(2)]
+        xc = [xpool.tile([P, NPATCH], U32, name="xc%d" % g, align_bytes=64) for g in range(2)]
+        xs = [xpool.tile([P, NPATCH], U8, name="xs%d" % g, align_bytes=64) for g in range(2)]
+        xt = {}
+
+        def x_reorder(h, q, copy):
             src = xn[h][:].bitcast(F32).rearrange("p (r j s) -> p j r s", r=16, j=16, s=8)
-            xr = xpool.tile([P, 2048], F32, name="xr%d" % h)
-            xr_v = xr[:].rearrange("p (j r s) -> p j r s", j=16, r=16, s=8)
-            xg = [xpool.tile([P, 2048], BF16, name="xg%d_%d" % (h, g), align_bytes=64) for g in range(2)]
-            for q in range(4):
-                js = slice(4 * q, 4 * q + 4)
-                if q == 1:
-                    nc.scalar.copy(out=xr_v[:, js], in_=src[:, js])
-                else:
-                    nc.vector.tensor_copy(out=xr_v[:, js], in_=src[:, js])
-            for q in range(4):
-                xt = ps_tp.tile([P, 4, P], F32, name="xt", tag="tp")
-                for jj in range(4):
-                    j = 4 * q + jj
-                    nc.tensor.transpose(out=xt[:, jj, :], in_=xr[:, j * P : (j + 1) * P], identity=ident[:])
-                xt_v = xt[:].rearrange("p j (c y) -> p j c y", c=4)
-                for g in range(2):
-                    dst = xg[g][:].bitcast(F32).rearrange("p (j y u) -> p j y u", j=16, y=YB, u=2)[:, 4 * q : 4 * q + 4]
-                    piece = xt_v[:, :, 2 * g : 2 * g + 2, :].rearrange("p j u y -> p j y u")
-                    if q % 2 == 0:
-                        nc.vector.tensor_copy(out=dst, in_=piece)
-                    else:
-                        nc.scalar.copy(out=dst, in_=piece)
-            for g in range(2):
-                codes = xpool.tile([P, COLS], U32, name="xc%d_%d" % (h, g), align_bytes=64)
-                scales = xpool.tile([P, COLS], U8, name="xs%d_%d" % (h, g), align_bytes=64)
-                nc.vector.quantize_mx(out=codes[:].bitcast(FP8X4), scales=scales[:], in_=xg[g][:])
-                xc[(h, g)] = codes
-                xs[(h, g)] = scales
+            dst = xr[h][:].rearrange("p (j r s) -> p j r s", j=16, r=16, s=8)
+            copy(out=dst[:, 4 * q : 4 * q + 4], in_=src[:, 4 * q : 4 * q + 4])
 
+        def x_transpose(h, q):
+            t = bank(("tp", "acc0", "acc1", "acc2")[q])
+            for jj in range(4):
+                j = 4 * q + jj
+                nc.tensor.transpose(out=t[:, jj, :], in_=xr[h][:, j * P : (j + 1) * P], identity=perm[:])
+            xt[(h, q)] = t
+
+        def x_evac(h, q, copy):
+            src = xt[(h, q)][:].rearrange("p j (g i f) -> p j g i f", g=2, i=16, f=4)
+            for g in range(2):
+                dst = xg[g][:].bitcast(F32).rearrange("p (j i h f) -> p j i h f", j=16, i=16, h=2, f=4)
+                copy(out=dst[:, 4 * q : 4 * q + 4, :, h, :], in_=src[:, :, g])
+
+        def x_quant(half, g):
+            nc.vector.quantize_mx(
+                out=xc[g][:, half * BANK : (half + 1) * BANK].bitcast(FP8X4),
+                scales=xs[g][:, half * BANK : (half + 1) * BANK],
+                in_=xg[g][:, half * 4 * BANK : (half + 1) * 4 * BANK],
+            )
+
+        wg = {}
         wc = {}
         ws = {}
         SECTION = (1, 2, 0)
 
-        def w_prep(c):
-            wg = wgrp.tile([P, 3072], BF16, name="wg", tag="wg", align_bytes=64)
-            wg_v = wg[:].bitcast(F32).rearrange("p (t g o u) -> p t g o u", t=3, g=2, o=P, u=2)
+        def w_transpose(c, copies):
+            wg[c] = wgrp.tile([P, 3072], BF16, name="wg", tag="wg", align_bytes=64)
+            wg_v = wg[c][:].bitcast(F32).rearrange("p (t g o u) -> p t g o u", t=3, g=2, o=P, u=2)
             for t in range(3):
-                wt = ps_tp.tile([P, 4, P], F32, name="wt", tag="tp")
+                wt = bank("tp")
                 words = wn[c][:, SECTION[t], :].bitcast(F32)
                 for chn in range(4):
                     nc.tensor.transpose(out=wt[:, chn, :], in_=words[:, chn * P : (chn + 1) * P], identity=ident[:])
-                nc.scalar.copy(out=wg_v[:, t], in_=wt[:].rearrange("p (g u) o -> p g o u", g=2, u=2))
-            codes = wq.tile([P, 768], U32, name="wc", tag="wc", align_bytes=64)
-            scales = wq.tile([P, 768], U8, name="ws", tag="ws", align_bytes=64)
-            nc.vector.quantize_mx(out=codes[:, 0:512].bitcast(FP8X4), scales=scales[:, 0:512], in_=wg[:, 0:2048])
-            nc.vector.quantize_mx(out=codes[:, 512:768].bitcast(FP8X4), scales=scales[:, 512:768], in_=wg[:, 2048:3072])
-            wc[c] = codes
-            ws[c] = scales
+                copies[t](out=wg_v[:, t], in_=wt[:].rearrange("p (g u) o -> p g o u", g=2, u=2))
 
-        def mx(c, h, t):
-            acc = ps_mx.tile([P, COLS], F32, name="acc", tag="acc%d" % t)
+        def w_quant_kv(c):
+            wc[c] = wq.tile([P, 768], U32, name="wc", tag="wc", align_bytes=64)
+            ws[c] = wq.tile([P, 768], U8, name="ws", tag="ws", align_bytes=64)
+            nc.vector.quantize_mx(out=wc[c][:, 0:512].bitcast(FP8X4), scales=ws[c][:, 0:512], in_=wg[c][:, 0:2048])
+
+        def w_quant_q(c):
+            nc.vector.quantize_mx(
+                out=wc[c][:, 512:768].bitcast(FP8X4), scales=ws[c][:, 512:768], in_=wg[c][:, 2048:3072]
+            )
+
+        def mx(c, half, t):
+            acc = ps_mx.tile([P, BANK], F32, name="acc", tag="acc%d" % t)
             for g in range(2):
                 cols = slice(t * 256 + g * P, t * 256 + (g + 1) * P)
+                pats = slice(half * BANK, (half + 1) * BANK)
                 nc.tensor.matmul_mx(
                     out=acc[:],
                     lhsT=wc[c][:, cols].bitcast(FP8X4),
                     lhsT_scale=ws[c][:, cols],
-                    rhs=xc[(h, g)][:].bitcast(FP8X4),
-                    rhs_scale=xs[(h, g)][:],
+                    rhs=xc[g][:, pats].bitcast(FP8X4),
+                    rhs_scale=xs[g][:, pats],
                     start=(g == 0),
                     stop=(g == 1),
                 )
             return acc
 
-        k_sb = {}
+        ks = {}
         v_ps = {}
+        q_ps = {}
         kv = {}
         tt = {}
+        pt = {}
+        qt = {}
+        ut = {}
+        o_tiles = {}
+        os_tiles = {}
 
-        def front(c, h):
-            k_ps = mx(c, h, 0)
-            v_ps[(c, h)] = mx(c, h, 1)
-            ks = work.tile([P, COLS], F32, name="ks", tag="ks%d" % h)
-            nc.scalar.activation(out=ks[:], in_=k_ps[:], func=ACT.Identity, bias=bias[:, 8 + c : 9 + c], scale=1.0)
-            k_sb[(c, h)] = ks
-            kvt = work.tile([P, 18, YB], F32, name="kvt", tag="kv%d" % h)
+        def borders(c):
+            kv[c] = work2.tile([P, 18, YJ], F32, name="kv", tag="kv")
             nc.scalar.activation(
-                out=kvt[:, 0:18:17, :],
-                in_=ones[:, 0:64].rearrange("p (a y) -> p a y", a=2),
+                out=kv[c][:, 0:18:17, :],
+                in_=ones[:].rearrange("p (a y) -> p a y", a=2),
                 func=ACT.Copy,
                 scale=cb[:, c : c + 1],
             )
-            kv[(c, h)] = kvt
-            ttt = work.tile([P, 16, TROW], F32, name="ttt", tag="tt%d" % h)
+            tt[c] = work2.tile([P, 16, TROW], F32, name="tt", tag="tt")
             nc.scalar.activation(
-                out=ttt[:].rearrange("p j (l f) -> p j l f", f=4)[:, :, 1:11:9, :],
+                out=tt[c][:].rearrange("p j (l f) -> p j l f", f=4)[:, :, 1:19:17, :],
                 in_=ones[:].rearrange("p (j l f) -> p j l f", j=16, l=2, f=4),
                 func=ACT.Copy,
                 scale=cbh[:, c : c + 1],
             )
-            tt[(c, h)] = ttt
 
-        o_tiles = {}
+        def front(c):
+            ks[c] = work2.tile([P, NPATCH], F32, name="ks", tag="ks")
+            for half in range(2):
+                k_ps = mx(c, half, 0)
+                v_ps[(c, half)] = mx(c, half, 1)
+                nc.scalar.activation(
+                    out=ks[c][:, half * BANK : (half + 1) * BANK], in_=k_ps[:], func=ACT.Identity,
+                    bias=bias[:, 8 + c : 9 + c], scale=1.0,
+                )
 
-        def chunk(c):
+        def stt(o, a, s, b, op0, op1):
+            nc.vector.scalar_tensor_tensor(out=o, in0=a, scalar=s, in1=b, op0=op0, op1=op1)
+
+        def st_k(c, half):
+            flat = kv[c][:].rearrange("p a y -> p (a y)")
+            stt(
+                flat[:, YJ + half * BANK : YJ + (half + 1) * BANK], v_ps[(c, half)][:], bias[:, 16 + c : 17 + c],
+                ks[c][:, half * BANK : (half + 1) * BANK], ALU.add, ALU.mult,
+            )
+
+        def st_h1(c):
+            flat = kv[c][:].rearrange("p a y -> p (a y)")
+            pt[c] = work1.tile([P, 16, YJ], F32, name="pt", tag="pt")
+            stt(
+                pt[c][:].rearrange("p j y -> p (j y)"), flat[:, 0:NPATCH], tab[:, 0:1], flat[:, YJ : YJ + NPATCH],
+                ALU.mult, ALU.add,
+            )
+
+        def st_h2(c):
+            stt(tt[c][:, :, 8:72], kv[c][:, 2:18, :], tab[:, 1:2], pt[c][:], ALU.mult, ALU.add)
+
+        def st_v1(c, js):
+            rh = c % 2
+            if c not in qt:
+                qt[c] = work1.tile([P, 16, YJ], F32, name="qt", tag="qt")
+            stt(qt[c][:, js, :], tt[c][:, js, 4:68], tab[:, 2 + rh : 3 + rh], tt[c][:, js, 8:72], ALU.mult, ALU.add)
+
+        def st_v2(c, js):
+            rh = c % 2
+            if c not in ut:
+                ut[c] = work1.tile([P, 16, YJ], F32, name="ut", tag="ut")
+            stt(ut[c][:, js, :], tt[c][:, js, 12:76], tab[:, 4 + rh : 5 + rh], qt[c][:, js, :], ALU.mult, ALU.add)
+
+        def st_f(c, half):
             ch = c // 2
             rh = c % 2
-            halves = range(NHALF)
-            for h in halves:
-                flat = kv[(c, h)][:].rearrange("p a y -> p (a y)")
-                nc.vector.scalar_tensor_tensor(
-                    out=flat[:, YB : YB + COLS],
-                    in0=v_ps[(c, h)][:],
-                    scalar=bias[:, 16 + c : 17 + c],
-                    in1=k_sb[(c, h)][:],
-                    op0=ALU.add,
-                    op1=ALU.mult,
+            if ch not in o_tiles:
+                o_tiles[ch] = outp.tile([P, 2048], F32, name="ot", tag="ot")
+            o_v = o_tiles[ch][:].rearrange("p (n a b) -> p n a b", a=2, b=4)
+            stt(
+                o_v[:, half * P : (half + 1) * P, rh, :],
+                q_ps[(c, half)][:].rearrange("p (n b) -> p n b", b=4),
+                bias[:, c : c + 1],
+                ut[c][:].rearrange("p j (i b) -> p (j i) b", b=4)[:, half * P : (half + 1) * P, :],
+                ALU.add, ALU.mult,
+            )
+
+        def out_bank(ch, q, copy, tag):
+            if ch not in os_tiles:
+                os_tiles[ch] = outp.tile([P, 8, 16, 16], F32, name="os_t", tag="os")
+            tp = bank(tag)
+            for jj in range(4):
+                j = 4 * q + jj
+                nc.tensor.transpose(out=tp[:, jj, :], in_=o_tiles[ch][:, j * P : (j + 1) * P], identity=ident[:])
+            copy(
+                out=os_tiles[ch][:, :, 4 * q : 4 * q + 4, :],
+                in_=tp[:].rearrange("p j (r s) -> p r j s", r=8, s=16),
+            )
+
+        def out_store(ch):
+            os_flat = os_tiles[ch][:].rearrange("p r j s -> p (r j s)")
+            for b in range(4):
+                nc.sync.dma_start(
+                    out=out[b, ch].rearrange("(m r) w -> m (r w)", r=8), in_=os_flat[b : b + 125 : 4, :]
                 )
-            q_ps = [mx(c, h, 2) for h in halves]
+
+        ALLJ = slice(0, 16)
+
+        x_reorder(0, 0, vcopy)
+        x_reorder(0, 1, vcopy)
+        x_reorder(0, 2, scopy)
+        x_reorder(0, 3, vcopy)
+        for q in range(4):
+            x_transpose(0, q)
+            x_evac(0, q, vcopy if q % 2 == 0 else scopy)
+        bias_columns()
+        borders(0)
+        x_reorder(1, 0, vcopy)
+        x_reorder(1, 1, scopy)
+        x_reorder(1, 2, vcopy)
+        x_transpose(1, 0)
+        x_evac(1, 0, vcopy)
+        x_reorder(1, 3, vcopy)
+        x_transpose(1, 1)
+        x_evac(1, 1, scopy)
+        x_quant(0, 0)
+        x_quant(0, 1)
+        x_transpose(1, 2)
+        x_evac(1, 2, scopy)
+        x_transpose(1, 3)
+        x_evac(1, 3, vcopy)
+        w_transpose(0, (scopy, scopy, scopy))
+        w_quant_kv(0)
+        x_quant(1, 0)
+        x_quant(1, 1)
+        w_quant_q(0)
+        front(0)
+        w_transpose(1, (scopy, scopy, scopy))
+        w_transpose(2, (scopy, scopy, scopy))
+
+        for c in range(NCHUNK + 1):
+            if c >= 1:
+                for half in range(2):
+                    q_ps[(c - 1, half)] = mx(c - 1, half, 2)
+            if c == 0:
+                st_k(0, 0)
+                w_quant_kv(1)
+                st_k(0, 1)
+                w_quant_q(1)
+            elif c < NCHUNK:
+                st_k(c, 0)
+                st_v1(c - 1, ALLJ)
+                st_k(c, 1)
+                st_v2(c - 1, ALLJ)
+            else:
+                st_v1(c - 1, slice(0, 8))
+                st_v1(c - 1, slice(8, 16))
+                st_v2(c - 1, slice(0, 8))
+                st_v2(c - 1, slice(8, 16))
             if c + 1 < NCHUNK:
-                for h in halves:
-                    front(c + 1, h)
-            pp = []
-            for h in halves:
-                flat = kv[(c, h)][:].rearrange("p a y -> p (a y)")
-                pt = work.tile([P, COLS], F32, name="pt", tag="pt%d" % h)
-                nc.vector.scalar_tensor_tensor(
-                    out=pt[:], in0=flat[:, 0:COLS], scalar=tab[:, 0:1], in1=flat[:, YB : YB + COLS],
-                    op0=ALU.mult, op1=ALU.add,
-                )
-                pp.append(pt)
-            for h in halves:
-                nc.vector.scalar_tensor_tensor(
-                    out=tt[(c, h)][:, :, 8:40],
-                    in0=kv[(c, h)][:, 2:18, :],
-                    scalar=tab[:, 1:2],
-                    in1=pp[h][:].rearrange("p (j y) -> p j y", y=YB),
-                    op0=ALU.mult, op1=ALU.add,
-                )
-            qq = []
-            for h in halves:
-                qt = work.tile([P, 16, YB], F32, name="qt", tag="qt%d" % h)
-                nc.vector.scalar_tensor_tensor(
-                    out=qt[:], in0=tt[(c, h)][:, :, 6:38], scalar=tab[:, 2 + rh : 3 + rh], in1=tt[(c, h)][:, :, 8:40],
-                    op0=ALU.mult, op1=ALU.add,
-                )
-                qq.append(qt)
-            uu = []
-            for h in halves:
-                ut = work.tile([P, 16, YB], F32, name="ut", tag="ut%d" % h)
-                nc.vector.scalar_tensor_tensor(
-                    out=ut[:], in0=tt[(c, h)][:, :, 10:42], scalar=tab[:, 4 + rh : 5 + rh], in1=qq[h][:],
-                    op0=ALU.mult, op1=ALU.add,
-                )
-                uu.append(ut)
-            if c + 2 < NCHUNK:
-                w_prep(c + 2)
-            if rh == 0:
-                o_tiles[ch] = outp.tile([P, 16, 2, NHALF, YB], F32, name="ot", tag="ot")
-            for h in halves:
-                nc.vector.scalar_tensor_tensor(
-                    out=o_tiles[ch][:, :, rh, h, :],
-                    in0=q_ps[h][:].rearrange("p (j y) -> p j y", y=YB),
-                    scalar=bias[:, c : c + 1],
-                    in1=uu[h][:],
-                    op0=ALU.add, op1=ALU.mult,
-                )
-            if rh == 1:
-                store(ch)
-
-        def store(ch):
-            o_flat = o_tiles[ch][:].rearrange("p j a h y -> p (j a h y)")
-            os_t = outp.tile([P, 8, 16, 16], F32, name="os_t", tag="os")
-            for q in range(4):
-                tp = ps_tp.tile([P, 4, P], F32, name="tp", tag="tp")
-                for jj in range(4):
-                    j = 4 * q + jj
-                    nc.tensor.transpose(out=tp[:, jj, :], in_=o_flat[:, j * P : (j + 1) * P], identity=ident[:])
-                nc.scalar.copy(
-                    out=os_t[:, :, 4 * q : 4 * q + 4, :],
-                    in_=tp[:].rearrange("p j (r s) -> p r j s", r=8, s=16),
-                )
-            os_flat = os_t[:].rearrange("p r j s -> p (r j s)")
-            for rh in range(2):
-                for h in range(NHALF):
-                    for bl in range(2):
-                        base = rh * 64 + h * 32 + bl
-                        nc.sync.dma_start(
-                            out=out[2 * h + bl, ch].rearrange("(i a r) w -> a i (r w)", a=2, r=8)[rh],
-                            in_=os_flat[base : base + 31 : 2, :],
-                        )
-
-        x_prep(0)
-        w_prep(0)
-        front(0, 0)
-        x_prep(1)
-        front(0, 1)
-        w_prep(1)
-        for c in range(NCHUNK):
-            chunk(c)
+                borders(c + 1)
+                front(c + 1)
+            if c == 0:
+                st_h1(0)
+                w_quant_kv(2)
+                st_h2(0)
+                w_quant_q(2)
+            elif c < NCHUNK:
+                st_h1(c)
+                st_f(c - 1, 0)
+                st_h2(c)
+                st_f(c - 1, 1)
+                if c + 2 < NCHUNK:
+                    w_quant_kv(c + 2)
+                    w_quant_q(c + 2)
+            else:
+                st_f(c - 1, 0)
+                out_bank(3, 0, scopy, "tp")
+                out_bank(3, 1, scopy, "tp")
+                st_f(c - 1, 1)
+                out_bank(3, 2, vcopy, "acc0")
+                out_bank(3, 3, scopy, "acc1")
+                out_store(3)
+            if c >= 3 and c % 2 == 1:
+                ch = (c - 3) // 2
+                for q in range(4):
+                    out_bank(ch, q, scopy, "tp")
+                out_store(ch)
+            if c + 3 < NCHUNK:
+                w_transpose(c + 3, (scopy, scopy, scopy))

@@ -20,6 +20,7 @@ NPATCH = 1024
 BANK = 512
 YJ = 64
 TROW = 80
+GP_J = 12
 
 
 def tile_attentionconv_kernel(tc, x, W_qkv, b_qkv, out):
@@ -28,13 +29,12 @@ def tile_attentionconv_kernel(tc, x, W_qkv, b_qkv, out):
         const = ctx.enter_context(tc.tile_pool(name="const", bufs=1))
         xpool = ctx.enter_context(tc.tile_pool(name="xpool", bufs=1))
         wnat = ctx.enter_context(tc.tile_pool(name="wnat", bufs=NCHUNK))
-        wgrp = ctx.enter_context(tc.tile_pool(name="wgrp", bufs=2))
-        wq = ctx.enter_context(tc.tile_pool(name="wq", bufs=4))
+        work3 = ctx.enter_context(tc.tile_pool(name="work3", bufs=3))
         work2 = ctx.enter_context(tc.tile_pool(name="work2", bufs=2))
         work1 = ctx.enter_context(tc.tile_pool(name="work1", bufs=1))
-        outp = ctx.enter_context(tc.tile_pool(name="outp", bufs=2))
         ps_mx = ctx.enter_context(tc.psum_pool(name="ps_mx", bufs=2))
         ps_tp = ctx.enter_context(tc.psum_pool(name="ps_tp", bufs=2))
+        ctx.enter_context(tc.manual_schedule())
 
         vcopy = nc.vector.tensor_copy
         scopy = nc.scalar.copy
@@ -45,19 +45,29 @@ def tile_attentionconv_kernel(tc, x, W_qkv, b_qkv, out):
 
         b_rows = const.tile([24, P], BF16, name="b_rows")
         nc.sync.dma_start(out=b_rows[:], in_=b_qkv.rearrange("(t p) -> t p", p=P))
-
         x_rows = x.rearrange("b c (i r) w -> (b c i) (r w)", r=16)
-        xn = []
-        for h in range(2):
-            t = xpool.tile([P, 4096], BF16, name="xn%d" % h)
-            nc.sync.dma_start(out=t[:], in_=x_rows[h * P : (h + 1) * P, :])
-            xn.append(t)
         w_view = W_qkv.rearrange("(s c p) k -> c p s k", s=3, c=NCHUNK, p=P)
-        wn = []
-        for c in range(NCHUNK):
-            t = wnat.tile([P, 3, 1024], BF16, name="wn", tag="wn")
-            nc.sync.dma_start(out=t[:], in_=w_view[c])
-            wn.append(t)
+        xn = [xpool.tile([P, 4096], BF16, name="xn%d" % h) for h in range(2)]
+        wn = [wnat.tile([P, 3, 1024], BF16, name="wn", tag="wn") for c in range(NCHUNK)]
+
+        def load_x(h):
+            nc.sync.dma_start(out=xn[h][:], in_=x_rows[h * P : (h + 1) * P, :])
+
+        def load_kv(c):
+            nc.sync.dma_start(out=wn[c][:, 1:3, :], in_=w_view[c][:, 1:3, :])
+
+        def load_q(c):
+            nc.sync.dma_start(out=wn[c][:, 0:1, :], in_=w_view[c][:, 0:1, :])
+
+        load_x(0)
+        load_kv(0)
+        load_x(1)
+        load_kv(1)
+        load_q(0)
+        for c in range(2, NCHUNK):
+            load_kv(c)
+            load_q(c - 1)
+        load_q(NCHUNK - 1)
 
         ident = const.tile([P, P], F32, name="ident")
         make_identity(nc, ident[:])
@@ -88,44 +98,38 @@ def tile_attentionconv_kernel(tc, x, W_qkv, b_qkv, out):
         pm_v = perm[:].rearrange("p (g i bl u) -> p g i bl u", g=2, i=16, bl=2, u=2)
         for g in range(2):
             vcopy(out=pm_v[:, g], in_=id_v[:, g])
+        b_rows_f = const.tile([P, P], F32, name="b_rows_f")
+        nc.vector.memset(b_rows_f[:], 0.0)
         hs = const.tile([P, 1], F32, name="hs")
         nc.vector.scalar_tensor_tensor(
             out=hs[:], in0=tab[:, 0:1], scalar=1.0, in1=tab[:, 1:2], op0=ALU.add, op1=ALU.add
         )
-        b_rows_f = const.tile([P, P], F32, name="b_rows_f")
-        nc.vector.memset(b_rows_f[:], 0.0)
+        vcopy(out=b_rows_f[0:24, :], in_=b_rows[:])
+        b_ps = bank("tp")
+        nc.tensor.transpose(out=b_ps[:, 0, :], in_=b_rows_f[:], identity=ident[:])
         bias = const.tile([P, 24], F32, name="bias")
+        vcopy(out=bias[:], in_=b_ps[:, 0, 0:24])
         cb = const.tile([P, NCHUNK], F32, name="cb")
+        nc.vector.tensor_mul(out=cb[:], in0=bias[:, 8:16], in1=bias[:, 16:24])
         cbh = const.tile([P, NCHUNK], F32, name="cbh")
-
-        def bias_columns():
-            vcopy(out=b_rows_f[0:24, :], in_=b_rows[:])
-            b_ps = bank("tp")
-            nc.tensor.transpose(out=b_ps[:, 0, :], in_=b_rows_f[:], identity=ident[:])
-            vcopy(out=bias[:], in_=b_ps[:, 0, 0:24])
-            nc.vector.tensor_mul(out=cb[:], in0=bias[:, 8:16], in1=bias[:, 16:24])
-            nc.vector.tensor_scalar_mul(out=cbh[:], in0=cb[:], scalar1=hs[:, 0:1])
+        nc.vector.tensor_scalar_mul(out=cbh[:], in0=cb[:], scalar1=hs[:, 0:1])
 
         xr = [xpool.tile([P, 2048], F32, name="xr%d" % h) for h in range(2)]
         xg = [xpool.tile([P, 4096], BF16, name="xg%d" % g, align_bytes=64) for g in range(2)]
         xc = [xpool.tile([P, NPATCH], U32, name="xc%d" % g, align_bytes=64) for g in range(2)]
         xs = [xpool.tile([P, NPATCH], U8, name="xs%d" % g, align_bytes=64) for g in range(2)]
-        xt = {}
 
         def x_reorder(h, q, copy):
             src = xn[h][:].bitcast(F32).rearrange("p (r j s) -> p j r s", r=16, j=16, s=8)
             dst = xr[h][:].rearrange("p (j r s) -> p j r s", j=16, r=16, s=8)
             copy(out=dst[:, 4 * q : 4 * q + 4], in_=src[:, 4 * q : 4 * q + 4])
 
-        def x_transpose(h, q):
-            t = bank(("tp", "acc0", "acc1", "acc2")[q])
+        def x_bank(h, q, tag, copy):
+            t = bank(tag)
             for jj in range(4):
                 j = 4 * q + jj
                 nc.tensor.transpose(out=t[:, jj, :], in_=xr[h][:, j * P : (j + 1) * P], identity=perm[:])
-            xt[(h, q)] = t
-
-        def x_evac(h, q, copy):
-            src = xt[(h, q)][:].rearrange("p j (g i f) -> p j g i f", g=2, i=16, f=4)
+            src = t[:].rearrange("p j (g i f) -> p j g i f", g=2, i=16, f=4)
             for g in range(2):
                 dst = xg[g][:].bitcast(F32).rearrange("p (j i h f) -> p j i h f", j=16, i=16, h=2, f=4)
                 copy(out=dst[:, 4 * q : 4 * q + 4, :, h, :], in_=src[:, :, g])
@@ -137,40 +141,49 @@ def tile_attentionconv_kernel(tc, x, W_qkv, b_qkv, out):
                 in_=xg[g][:, half * 4 * BANK : (half + 1) * 4 * BANK],
             )
 
-        wg = {}
-        wc = {}
-        ws = {}
-        SECTION = (1, 2, 0)
+        wg_kv = {}
+        wg_q = {}
+        wc_kv = {}
+        ws_kv = {}
+        wc_q = {}
+        ws_q = {}
 
-        def w_transpose(c, copies):
-            wg[c] = wgrp.tile([P, 3072], BF16, name="wg", tag="wg", align_bytes=64)
-            wg_v = wg[c][:].bitcast(F32).rearrange("p (t g o u) -> p t g o u", t=3, g=2, o=P, u=2)
-            for t in range(3):
-                wt = bank("tp")
-                words = wn[c][:, SECTION[t], :].bitcast(F32)
-                for chn in range(4):
-                    nc.tensor.transpose(out=wt[:, chn, :], in_=words[:, chn * P : (chn + 1) * P], identity=ident[:])
-                copies[t](out=wg_v[:, t], in_=wt[:].rearrange("p (g u) o -> p g o u", g=2, u=2))
+        def w_bank(c, section, dst):
+            wt = bank("tp")
+            words = wn[c][:, section, :].bitcast(F32)
+            for chn in range(4):
+                nc.tensor.transpose(out=wt[:, chn, :], in_=words[:, chn * P : (chn + 1) * P], identity=ident[:])
+            scopy(out=dst, in_=wt[:].rearrange("p (g u) o -> p g o u", g=2, u=2))
+
+        def w_transpose_kv(c):
+            wg_kv[c] = work2.tile([P, 2048], BF16, name="wgkv", tag="wgkv", align_bytes=64)
+            v = wg_kv[c][:].bitcast(F32).rearrange("p (t g o u) -> p t g o u", t=2, g=2, o=P, u=2)
+            w_bank(c, 1, v[:, 0])
+            w_bank(c, 2, v[:, 1])
+
+        def w_transpose_q(c):
+            wg_q[c] = work2.tile([P, 1024], BF16, name="wgq", tag="wgq", align_bytes=64)
+            w_bank(c, 0, wg_q[c][:].bitcast(F32).rearrange("p (g o u) -> p g o u", g=2, o=P, u=2))
 
         def w_quant_kv(c):
-            wc[c] = wq.tile([P, 768], U32, name="wc", tag="wc", align_bytes=64)
-            ws[c] = wq.tile([P, 768], U8, name="ws", tag="ws", align_bytes=64)
-            nc.vector.quantize_mx(out=wc[c][:, 0:512].bitcast(FP8X4), scales=ws[c][:, 0:512], in_=wg[c][:, 0:2048])
+            wc_kv[c] = work3.tile([P, 512], U32, name="wckv", tag="wckv", align_bytes=64)
+            ws_kv[c] = work3.tile([P, 512], U8, name="wskv", tag="wskv", align_bytes=64)
+            nc.vector.quantize_mx(out=wc_kv[c][:].bitcast(FP8X4), scales=ws_kv[c][:], in_=wg_kv[c][:])
 
         def w_quant_q(c):
-            nc.vector.quantize_mx(
-                out=wc[c][:, 512:768].bitcast(FP8X4), scales=ws[c][:, 512:768], in_=wg[c][:, 2048:3072]
-            )
+            wc_q[c] = work3.tile([P, 256], U32, name="wcq", tag="wcq", align_bytes=64)
+            ws_q[c] = work3.tile([P, 256], U8, name="wsq", tag="wsq", align_bytes=64)
+            nc.vector.quantize_mx(out=wc_q[c][:].bitcast(FP8X4), scales=ws_q[c][:], in_=wg_q[c][:])
 
-        def mx(c, half, t):
-            acc = ps_mx.tile([P, BANK], F32, name="acc", tag="acc%d" % t)
+        def mx(codes, scales, first, half, tag):
+            acc = ps_mx.tile([P, BANK], F32, name="acc", tag=tag)
+            pats = slice(half * BANK, (half + 1) * BANK)
             for g in range(2):
-                cols = slice(t * 256 + g * P, t * 256 + (g + 1) * P)
-                pats = slice(half * BANK, (half + 1) * BANK)
+                cols = slice(first + g * P, first + (g + 1) * P)
                 nc.tensor.matmul_mx(
                     out=acc[:],
-                    lhsT=wc[c][:, cols].bitcast(FP8X4),
-                    lhsT_scale=ws[c][:, cols],
+                    lhsT=codes[:, cols].bitcast(FP8X4),
+                    lhsT_scale=scales[:, cols],
                     rhs=xc[g][:, pats].bitcast(FP8X4),
                     rhs_scale=xs[g][:, pats],
                     start=(g == 0),
@@ -185,6 +198,7 @@ def tile_attentionconv_kernel(tc, x, W_qkv, b_qkv, out):
         tt = {}
         pt = {}
         qt = {}
+        zt = {}
         ut = {}
         o_tiles = {}
         os_tiles = {}
@@ -197,7 +211,7 @@ def tile_attentionconv_kernel(tc, x, W_qkv, b_qkv, out):
                 func=ACT.Copy,
                 scale=cb[:, c : c + 1],
             )
-            tt[c] = work2.tile([P, 16, TROW], F32, name="tt", tag="tt")
+            tt[c] = work3.tile([P, 16, TROW], F32, name="tt", tag="tt")
             nc.scalar.activation(
                 out=tt[c][:].rearrange("p j (l f) -> p j l f", f=4)[:, :, 1:19:17, :],
                 in_=ones[:].rearrange("p (j l f) -> p j l f", j=16, l=2, f=4),
@@ -205,15 +219,19 @@ def tile_attentionconv_kernel(tc, x, W_qkv, b_qkv, out):
                 scale=cbh[:, c : c + 1],
             )
 
-        def front(c):
-            ks[c] = work2.tile([P, NPATCH], F32, name="ks", tag="ks")
+        def front(c, half):
+            if half == 0:
+                ks[c] = work2.tile([P, NPATCH], F32, name="ks", tag="ks")
+            k_ps = mx(wc_kv[c], ws_kv[c], 0, half, "acc0")
+            v_ps[(c, half)] = mx(wc_kv[c], ws_kv[c], 256, half, "acc1")
+            nc.scalar.activation(
+                out=ks[c][:, half * BANK : (half + 1) * BANK], in_=k_ps[:], func=ACT.Identity,
+                bias=bias[:, 8 + c : 9 + c], scale=1.0,
+            )
+
+        def mx_q(c):
             for half in range(2):
-                k_ps = mx(c, half, 0)
-                v_ps[(c, half)] = mx(c, half, 1)
-                nc.scalar.activation(
-                    out=ks[c][:, half * BANK : (half + 1) * BANK], in_=k_ps[:], func=ACT.Identity,
-                    bias=bias[:, 8 + c : 9 + c], scale=1.0,
-                )
+                q_ps[(c, half)] = mx(wc_q[c], ws_q[c], 0, half, "acc2")
 
         def stt(o, a, s, b, op0, op1):
             nc.vector.scalar_tensor_tensor(out=o, in0=a, scalar=s, in1=b, op0=op0, op1=op1)
@@ -236,23 +254,31 @@ def tile_attentionconv_kernel(tc, x, W_qkv, b_qkv, out):
         def st_h2(c):
             stt(tt[c][:, :, 8:72], kv[c][:, 2:18, :], tab[:, 1:2], pt[c][:], ALU.mult, ALU.add)
 
-        def st_v1(c, js):
+        def st_v1(c):
             rh = c % 2
-            if c not in qt:
-                qt[c] = work1.tile([P, 16, YJ], F32, name="qt", tag="qt")
-            stt(qt[c][:, js, :], tt[c][:, js, 4:68], tab[:, 2 + rh : 3 + rh], tt[c][:, js, 8:72], ALU.mult, ALU.add)
+            qt[c] = work2.tile([P, 16, YJ], F32, name="qt", tag="qt")
+            ut[c] = work2.tile([P, 16, YJ], F32, name="ut", tag="ut")
+            stt(qt[c][:], tt[c][:, :, 4:68], tab[:, 2 + rh : 3 + rh], tt[c][:, :, 8:72], ALU.mult, ALU.add)
+
+        def st_z(c):
+            rh = c % 2
+            zt[c] = work2.tile([P, GP_J, YJ], F32, name="zt", tag="zt")
+            nc.scalar.activation(
+                out=zt[c][:], in_=tt[c][:, 0:GP_J, 12:76], func=ACT.Copy, scale=tab[:, 4 + rh : 5 + rh]
+            )
+
+        def st_g(c):
+            nc.gpsimd.tensor_tensor(out=ut[c][:, 0:GP_J, :], in0=qt[c][:, 0:GP_J, :], in1=zt[c][:], op=ALU.add)
 
         def st_v2(c, js):
             rh = c % 2
-            if c not in ut:
-                ut[c] = work1.tile([P, 16, YJ], F32, name="ut", tag="ut")
             stt(ut[c][:, js, :], tt[c][:, js, 12:76], tab[:, 4 + rh : 5 + rh], qt[c][:, js, :], ALU.mult, ALU.add)
 
         def st_f(c, half):
             ch = c // 2
             rh = c % 2
             if ch not in o_tiles:
-                o_tiles[ch] = outp.tile([P, 2048], F32, name="ot", tag="ot")
+                o_tiles[ch] = work2.tile([P, 2048], F32, name="ot", tag="ot")
             o_v = o_tiles[ch][:].rearrange("p (n a b) -> p n a b", a=2, b=4)
             stt(
                 o_v[:, half * P : (half + 1) * P, rh, :],
@@ -264,7 +290,7 @@ def tile_attentionconv_kernel(tc, x, W_qkv, b_qkv, out):
 
         def out_bank(ch, q, copy, tag):
             if ch not in os_tiles:
-                os_tiles[ch] = outp.tile([P, 8, 16, 16], F32, name="os_t", tag="os")
+                os_tiles[ch] = work2.tile([P, 8, 16, 16], F32, name="os_t", tag="os")
             tp = bank(tag)
             for jj in range(4):
                 j = 4 * q + jj
@@ -281,87 +307,82 @@ def tile_attentionconv_kernel(tc, x, W_qkv, b_qkv, out):
                     out=out[b, ch].rearrange("(m r) w -> m (r w)", r=8), in_=os_flat[b : b + 125 : 4, :]
                 )
 
-        ALLJ = slice(0, 16)
-
-        x_reorder(0, 0, vcopy)
-        x_reorder(0, 1, vcopy)
-        x_reorder(0, 2, scopy)
-        x_reorder(0, 3, vcopy)
-        for q in range(4):
-            x_transpose(0, q)
-            x_evac(0, q, vcopy if q % 2 == 0 else scopy)
-        bias_columns()
         borders(0)
+        x_reorder(0, 0, vcopy)
+        x_reorder(0, 1, scopy)
+        x_reorder(0, 2, vcopy)
+        x_reorder(0, 3, vcopy)
+        x_bank(0, 0, "acc0", vcopy)
+        x_bank(0, 1, "acc0", scopy)
+        x_bank(0, 2, "acc1", vcopy)
+        x_bank(0, 3, "acc1", scopy)
         x_reorder(1, 0, vcopy)
         x_reorder(1, 1, scopy)
         x_reorder(1, 2, vcopy)
-        x_transpose(1, 0)
-        x_evac(1, 0, vcopy)
         x_reorder(1, 3, vcopy)
-        x_transpose(1, 1)
-        x_evac(1, 1, scopy)
+        w_transpose_kv(0)
+        x_bank(1, 0, "acc2", vcopy)
+        x_bank(1, 1, "acc2", scopy)
+        w_quant_kv(0)
         x_quant(0, 0)
         x_quant(0, 1)
-        x_transpose(1, 2)
-        x_evac(1, 2, scopy)
-        x_transpose(1, 3)
-        x_evac(1, 3, vcopy)
-        w_transpose(0, (scopy, scopy, scopy))
-        w_quant_kv(0)
+        x_bank(1, 2, "acc0", scopy)
+        x_bank(1, 3, "acc1", scopy)
+        w_transpose_kv(1)
+        front(0, 0)
         x_quant(1, 0)
         x_quant(1, 1)
-        w_quant_q(0)
-        front(0)
-        w_transpose(1, (scopy, scopy, scopy))
-        w_transpose(2, (scopy, scopy, scopy))
+        front(0, 1)
+        w_quant_kv(1)
+        w_transpose_kv(2)
+        w_transpose_q(0)
 
-        for c in range(NCHUNK + 1):
-            if c >= 1:
-                for half in range(2):
-                    q_ps[(c - 1, half)] = mx(c - 1, half, 2)
-            if c == 0:
-                st_k(0, 0)
-                w_quant_kv(1)
-                st_k(0, 1)
-                w_quant_q(1)
-            elif c < NCHUNK:
-                st_k(c, 0)
-                st_v1(c - 1, ALLJ)
-                st_k(c, 1)
-                st_v2(c - 1, ALLJ)
-            else:
-                st_v1(c - 1, slice(0, 8))
-                st_v1(c - 1, slice(8, 16))
-                st_v2(c - 1, slice(0, 8))
-                st_v2(c - 1, slice(8, 16))
-            if c + 1 < NCHUNK:
-                borders(c + 1)
-                front(c + 1)
-            if c == 0:
-                st_h1(0)
-                w_quant_kv(2)
-                st_h2(0)
-                w_quant_q(2)
-            elif c < NCHUNK:
-                st_h1(c)
-                st_f(c - 1, 0)
-                st_h2(c)
-                st_f(c - 1, 1)
-                if c + 2 < NCHUNK:
-                    w_quant_kv(c + 2)
-                    w_quant_q(c + 2)
-            else:
-                st_f(c - 1, 0)
+        last = NCHUNK - 1
+        for p in range(NCHUNK + 2):
+            if p <= last:
+                st_k(p, 0)
+                st_k(p, 1)
+            if 1 <= p <= last and GP_J > 0:
+                st_g(p - 1)
+            if 2 <= p <= last + 1:
+                st_f(p - 2, 0)
+                st_f(p - 2, 1)
+            if p == last + 2:
+                st_f(last, 0)
                 out_bank(3, 0, scopy, "tp")
                 out_bank(3, 1, scopy, "tp")
-                st_f(c - 1, 1)
+                st_f(last, 1)
                 out_bank(3, 2, vcopy, "acc0")
                 out_bank(3, 3, scopy, "acc1")
                 out_store(3)
-            if c >= 3 and c % 2 == 1:
-                ch = (c - 3) // 2
+            if p + 1 <= last:
+                borders(p + 1)
+                front(p + 1, 0)
+                front(p + 1, 1)
+            if 1 <= p <= last + 1:
+                mx_q(p - 1)
+            if p <= last:
+                st_h1(p)
+            if 1 <= p <= last and GP_J < 16:
+                st_v2(p - 1, slice(GP_J, 16))
+            if p == last + 1:
+                st_v2(last, slice(0, 8))
+                st_v2(last, slice(8, 16))
+            if p <= last:
+                st_h2(p)
+            if p < last and GP_J > 0:
+                st_z(p)
+            if p in (3, 5, 7):
+                ch = (p - 3) // 2
                 for q in range(4):
                     out_bank(ch, q, scopy, "tp")
                 out_store(ch)
-            if c + 3 < NCHUNK:
-                w_transpose(c + 3, (scopy, scopy, scopy))
+            if p + 2 <= last:
+                w_quant_kv(p + 2)
+            if p <= last:
+                w_quant_q(p)
+                st_v1(p)
+            if p + 3 <= last:
+                w_transpose_kv(p + 3)
+            if p + 1 <= last:
+                w_transpose_q(p + 1)

@@ -134,12 +134,13 @@ def tile_attentionconv_kernel(tc, x, W_qkv, b_qkv, out):
                 dst = xg[g][:].bitcast(F32).rearrange("p (j i h f) -> p j i h f", j=16, i=16, h=2, f=4)
                 copy(out=dst[:, 4 * q : 4 * q + 4, :, h, :], in_=src[:, :, g])
 
-        def x_quant(half, g):
-            nc.vector.quantize_mx(
-                out=xc[g][:, half * BANK : (half + 1) * BANK].bitcast(FP8X4),
-                scales=xs[g][:, half * BANK : (half + 1) * BANK],
-                in_=xg[g][:, half * 4 * BANK : (half + 1) * 4 * BANK],
-            )
+        def x_quant(q):
+            for g in range(2):
+                nc.vector.quantize_mx(
+                    out=xc[g][:, q * 256 : (q + 1) * 256].bitcast(FP8X4),
+                    scales=xs[g][:, q * 256 : (q + 1) * 256],
+                    in_=xg[g][:, q * 1024 : (q + 1) * 1024],
+                )
 
         wg_kv = {}
         wg_q = {}
@@ -274,17 +275,18 @@ def tile_attentionconv_kernel(tc, x, W_qkv, b_qkv, out):
             rh = c % 2
             stt(ut[c][:, js, :], tt[c][:, js, 12:76], tab[:, 4 + rh : 5 + rh], qt[c][:, js, :], ALU.mult, ALU.add)
 
-        def st_f(c, half):
+        def st_f(c, first, count):
             ch = c // 2
             rh = c % 2
             if ch not in o_tiles:
                 o_tiles[ch] = work2.tile([P, 2048], F32, name="ot", tag="ot")
             o_v = o_tiles[ch][:].rearrange("p (n a b) -> p n a b", a=2, b=4)
+            inside = first % P
             stt(
-                o_v[:, half * P : (half + 1) * P, rh, :],
-                q_ps[(c, half)][:].rearrange("p (n b) -> p n b", b=4),
+                o_v[:, first : first + count, rh, :],
+                q_ps[(c, first // P)][:].rearrange("p (n b) -> p n b", b=4)[:, inside : inside + count, :],
                 bias[:, c : c + 1],
-                ut[c][:].rearrange("p j (i b) -> p (j i) b", b=4)[:, half * P : (half + 1) * P, :],
+                ut[c][:].rearrange("p j (i b) -> p (j i) b", b=4)[:, first : first + count, :],
                 ALU.add, ALU.mult,
             )
 
@@ -307,6 +309,14 @@ def tile_attentionconv_kernel(tc, x, W_qkv, b_qkv, out):
                     out=out[b, ch].rearrange("(m r) w -> m (r w)", r=8), in_=os_flat[b : b + 125 : 4, :]
                 )
 
+        def out_store_half(ch, half):
+            os_rows = os_tiles[ch][:].rearrange("p r j s -> p r (j s)")
+            cols = slice(half * P, (half + 1) * P)
+            for b in range(4):
+                nc.sync.dma_start(
+                    out=out[b, ch].rearrange("(m r) w -> m r w", r=8)[:, :, cols], in_=os_rows[b : b + 125 : 4, :, cols]
+                )
+
         borders(0)
         x_reorder(0, 0, vcopy)
         x_reorder(0, 1, scopy)
@@ -324,14 +334,14 @@ def tile_attentionconv_kernel(tc, x, W_qkv, b_qkv, out):
         x_bank(1, 0, "acc2", vcopy)
         x_bank(1, 1, "acc2", scopy)
         w_quant_kv(0)
-        x_quant(0, 0)
-        x_quant(0, 1)
+        x_quant(0)
+        x_quant(1)
         x_bank(1, 2, "acc0", scopy)
         x_bank(1, 3, "acc1", scopy)
         w_transpose_kv(1)
         front(0, 0)
-        x_quant(1, 0)
-        x_quant(1, 1)
+        x_quant(2)
+        x_quant(3)
         front(0, 1)
         w_quant_kv(1)
         w_transpose_kv(2)
@@ -345,16 +355,19 @@ def tile_attentionconv_kernel(tc, x, W_qkv, b_qkv, out):
             if 1 <= p <= last and GP_J > 0:
                 st_g(p - 1)
             if 2 <= p <= last + 1:
-                st_f(p - 2, 0)
-                st_f(p - 2, 1)
+                st_f(p - 2, 0, P)
+                st_f(p - 2, P, P)
             if p == last + 2:
-                st_f(last, 0)
+                st_f(last, 0, 64)
                 out_bank(3, 0, scopy, "tp")
+                st_f(last, 64, 64)
                 out_bank(3, 1, scopy, "tp")
-                st_f(last, 1)
-                out_bank(3, 2, vcopy, "acc0")
-                out_bank(3, 3, scopy, "acc1")
-                out_store(3)
+                out_store_half(3, 0)
+                st_f(last, 128, 64)
+                out_bank(3, 2, scopy, "acc0")
+                st_f(last, 192, 64)
+                out_bank(3, 3, vcopy, "acc1")
+                out_store_half(3, 1)
             if p + 1 <= last:
                 borders(p + 1)
                 front(p + 1, 0)

@@ -20,6 +20,8 @@ NPATCH = 1024
 BANK = 512
 YJ = 64
 TROW = 80
+WARM_FIRST = 12
+WARM_LATER = 3
 GP_J = 12
 
 
@@ -43,8 +45,18 @@ def tile_attentionconv_kernel(tc, x, W_qkv, b_qkv, out):
             pool = ps_tp if tag == "tp" else ps_mx
             return pool.tile([P, 4, P], F32, name="bk", tag=tag)
 
+        warm = const.tile([P, BANK], BF16, name="warm")
+        nc.vector.memset(warm[:], 0.0)
+
+        def keep_warm(n):
+            wp = ps_mx.tile([P, BANK], F32, name="wp", tag="acc2")
+            for k in range(n):
+                nc.tensor.matmul(out=wp[:], lhsT=warm[:, 0:P], rhs=warm[:], start=True, stop=True)
+
+        keep_warm(WARM_FIRST)
+
         b_rows = const.tile([24, P], BF16, name="b_rows")
-        nc.sync.dma_start(out=b_rows[:], in_=b_qkv.rearrange("(t p) -> t p", p=P))
+        nc.scalar.dma_start(out=b_rows[:], in_=b_qkv.rearrange("(t p) -> t p", p=P))
         x_rows = x.rearrange("b c (i r) w -> (b c i) (r w)", r=16)
         w_view = W_qkv.rearrange("(s c p) k -> c p s k", s=3, c=NCHUNK, p=P)
         xn = [xpool.tile([P, 4096], BF16, name="xn%d" % h) for h in range(2)]
@@ -134,13 +146,12 @@ def tile_attentionconv_kernel(tc, x, W_qkv, b_qkv, out):
                 dst = xg[g][:].bitcast(F32).rearrange("p (j i h f) -> p j i h f", j=16, i=16, h=2, f=4)
                 copy(out=dst[:, 4 * q : 4 * q + 4, :, h, :], in_=src[:, :, g])
 
-        def x_quant(q):
-            for g in range(2):
-                nc.vector.quantize_mx(
-                    out=xc[g][:, q * 256 : (q + 1) * 256].bitcast(FP8X4),
-                    scales=xs[g][:, q * 256 : (q + 1) * 256],
-                    in_=xg[g][:, q * 1024 : (q + 1) * 1024],
-                )
+        def x_quant(half, g):
+            nc.vector.quantize_mx(
+                out=xc[g][:, half * BANK : (half + 1) * BANK].bitcast(FP8X4),
+                scales=xs[g][:, half * BANK : (half + 1) * BANK],
+                in_=xg[g][:, half * 4 * BANK : (half + 1) * 4 * BANK],
+            )
 
         wg_kv = {}
         wg_q = {}
@@ -275,18 +286,17 @@ def tile_attentionconv_kernel(tc, x, W_qkv, b_qkv, out):
             rh = c % 2
             stt(ut[c][:, js, :], tt[c][:, js, 12:76], tab[:, 4 + rh : 5 + rh], qt[c][:, js, :], ALU.mult, ALU.add)
 
-        def st_f(c, first, count):
+        def st_f(c, half):
             ch = c // 2
             rh = c % 2
             if ch not in o_tiles:
                 o_tiles[ch] = work2.tile([P, 2048], F32, name="ot", tag="ot")
             o_v = o_tiles[ch][:].rearrange("p (n a b) -> p n a b", a=2, b=4)
-            inside = first % P
             stt(
-                o_v[:, first : first + count, rh, :],
-                q_ps[(c, first // P)][:].rearrange("p (n b) -> p n b", b=4)[:, inside : inside + count, :],
+                o_v[:, half * P : (half + 1) * P, rh, :],
+                q_ps[(c, half)][:].rearrange("p (n b) -> p n b", b=4),
                 bias[:, c : c + 1],
-                ut[c][:].rearrange("p j (i b) -> p (j i) b", b=4)[:, first : first + count, :],
+                ut[c][:].rearrange("p j (i b) -> p (j i) b", b=4)[:, half * P : (half + 1) * P, :],
                 ALU.add, ALU.mult,
             )
 
@@ -309,14 +319,6 @@ def tile_attentionconv_kernel(tc, x, W_qkv, b_qkv, out):
                     out=out[b, ch].rearrange("(m r) w -> m (r w)", r=8), in_=os_flat[b : b + 125 : 4, :]
                 )
 
-        def out_store_half(ch, half):
-            os_rows = os_tiles[ch][:].rearrange("p r j s -> p r (j s)")
-            cols = slice(half * P, (half + 1) * P)
-            for b in range(4):
-                nc.sync.dma_start(
-                    out=out[b, ch].rearrange("(m r) w -> m r w", r=8)[:, :, cols], in_=os_rows[b : b + 125 : 4, :, cols]
-                )
-
         borders(0)
         x_reorder(0, 0, vcopy)
         x_reorder(0, 1, scopy)
@@ -331,17 +333,19 @@ def tile_attentionconv_kernel(tc, x, W_qkv, b_qkv, out):
         x_reorder(1, 2, vcopy)
         x_reorder(1, 3, vcopy)
         w_transpose_kv(0)
+        keep_warm(WARM_LATER)
         x_bank(1, 0, "acc2", vcopy)
         x_bank(1, 1, "acc2", scopy)
         w_quant_kv(0)
-        x_quant(0)
-        x_quant(1)
+        x_quant(0, 0)
+        x_quant(0, 1)
         x_bank(1, 2, "acc0", scopy)
         x_bank(1, 3, "acc1", scopy)
         w_transpose_kv(1)
+        keep_warm(WARM_LATER)
         front(0, 0)
-        x_quant(2)
-        x_quant(3)
+        x_quant(1, 0)
+        x_quant(1, 1)
         front(0, 1)
         w_quant_kv(1)
         w_transpose_kv(2)
@@ -355,19 +359,16 @@ def tile_attentionconv_kernel(tc, x, W_qkv, b_qkv, out):
             if 1 <= p <= last and GP_J > 0:
                 st_g(p - 1)
             if 2 <= p <= last + 1:
-                st_f(p - 2, 0, P)
-                st_f(p - 2, P, P)
+                st_f(p - 2, 0)
+                st_f(p - 2, 1)
             if p == last + 2:
-                st_f(last, 0, 64)
+                st_f(last, 0)
                 out_bank(3, 0, scopy, "tp")
-                st_f(last, 64, 64)
                 out_bank(3, 1, scopy, "tp")
-                out_store_half(3, 0)
-                st_f(last, 128, 64)
-                out_bank(3, 2, scopy, "acc0")
-                st_f(last, 192, 64)
-                out_bank(3, 3, vcopy, "acc1")
-                out_store_half(3, 1)
+                st_f(last, 1)
+                out_bank(3, 2, vcopy, "acc0")
+                out_bank(3, 3, scopy, "acc1")
+                out_store(3)
             if p + 1 <= last:
                 borders(p + 1)
                 front(p + 1, 0)

@@ -20,9 +20,7 @@ NPATCH = 1024
 BANK = 512
 YJ = 64
 TROW = 80
-WARM_FIRST = 12
-WARM_LATER = 3
-GP_J = 12
+GP_J = 0
 
 
 def tile_attentionconv_kernel(tc, x, W_qkv, b_qkv, out):
@@ -45,18 +43,8 @@ def tile_attentionconv_kernel(tc, x, W_qkv, b_qkv, out):
             pool = ps_tp if tag == "tp" else ps_mx
             return pool.tile([P, 4, P], F32, name="bk", tag=tag)
 
-        warm = const.tile([P, BANK], BF16, name="warm")
-        nc.vector.memset(warm[:], 0.0)
-
-        def keep_warm(n):
-            wp = ps_mx.tile([P, BANK], F32, name="wp", tag="acc2")
-            for k in range(n):
-                nc.tensor.matmul(out=wp[:], lhsT=warm[:, 0:P], rhs=warm[:], start=True, stop=True)
-
-        keep_warm(WARM_FIRST)
-
         b_rows = const.tile([24, P], BF16, name="b_rows")
-        nc.scalar.dma_start(out=b_rows[:], in_=b_qkv.rearrange("(t p) -> t p", p=P))
+        nc.sync.dma_start(out=b_rows[:], in_=b_qkv.rearrange("(t p) -> t p", p=P))
         x_rows = x.rearrange("b c (i r) w -> (b c i) (r w)", r=16)
         w_view = W_qkv.rearrange("(s c p) k -> c p s k", s=3, c=NCHUNK, p=P)
         xn = [xpool.tile([P, 4096], BF16, name="xn%d" % h) for h in range(2)]
@@ -333,7 +321,6 @@ def tile_attentionconv_kernel(tc, x, W_qkv, b_qkv, out):
         x_reorder(1, 2, vcopy)
         x_reorder(1, 3, vcopy)
         w_transpose_kv(0)
-        keep_warm(WARM_LATER)
         x_bank(1, 0, "acc2", vcopy)
         x_bank(1, 1, "acc2", scopy)
         w_quant_kv(0)
@@ -342,7 +329,6 @@ def tile_attentionconv_kernel(tc, x, W_qkv, b_qkv, out):
         x_bank(1, 2, "acc0", scopy)
         x_bank(1, 3, "acc1", scopy)
         w_transpose_kv(1)
-        keep_warm(WARM_LATER)
         front(0, 0)
         x_quant(1, 0)
         x_quant(1, 1)

@@ -20,7 +20,7 @@ NPATCH = 1024
 BANK = 512
 YJ = 64
 TROW = 80
-GP_J = 0
+GP_J = 8
 
 
 def tile_attentionconv_kernel(tc, x, W_qkv, b_qkv, out):

from contextlib import ExitStack

import concourse.mybir as mybir
from concourse.masks import make_identity

F32 = mybir.dt.float32
BF16 = mybir.dt.bfloat16
U32 = mybir.dt.uint32
U8 = mybir.dt.uint8
I32 = mybir.dt.int32
FP8X4 = mybir.dt.float8_e4m3fn_x4
ALU = mybir.AluOpType
ACT = mybir.ActivationFunctionType

FLOPS = 2 * 1024 * 1024 * 3072

P = 128
NCHUNK = 8
NPATCH = 1024
BANK = 512
YJ = 64
TROW = 80
GP_J = 8


def tile_attentionconv_kernel(tc, x, W_qkv, b_qkv, out):
    nc = tc.nc
    with ExitStack() as ctx:
        const = ctx.enter_context(tc.tile_pool(name="const", bufs=1))
        xpool = ctx.enter_context(tc.tile_pool(name="xpool", bufs=1))
        wnat = ctx.enter_context(tc.tile_pool(name="wnat", bufs=NCHUNK))
        work3 = ctx.enter_context(tc.tile_pool(name="work3", bufs=3))
        work2 = ctx.enter_context(tc.tile_pool(name="work2", bufs=2))
        work1 = ctx.enter_context(tc.tile_pool(name="work1", bufs=1))
        ps_mx = ctx.enter_context(tc.psum_pool(name="ps_mx", bufs=2))
        ps_tp = ctx.enter_context(tc.psum_pool(name="ps_tp", bufs=2))
        ctx.enter_context(tc.manual_schedule())

        vcopy = nc.vector.tensor_copy
        scopy = nc.scalar.copy

        def bank(tag):
            pool = ps_tp if tag == "tp" else ps_mx
            return pool.tile([P, 4, P], F32, name="bk", tag=tag)

        b_rows = const.tile([24, P], BF16, name="b_rows")
        nc.sync.dma_start(out=b_rows[:], in_=b_qkv.rearrange("(t p) -> t p", p=P))
        x_rows = x.rearrange("b c (i r) w -> (b c i) (r w)", r=16)
        w_view = W_qkv.rearrange("(s c p) k -> c p s k", s=3, c=NCHUNK, p=P)
        xn = [xpool.tile([P, 4096], BF16, name="xn%d" % h) for h in range(2)]
        wn = [wnat.tile([P, 3, 1024], BF16, name="wn", tag="wn") for c in range(NCHUNK)]

        def load_x(h):
            nc.sync.dma_start(out=xn[h][:], in_=x_rows[h * P : (h + 1) * P, :])

        def load_kv(c):
            nc.sync.dma_start(out=wn[c][:, 1:3, :], in_=w_view[c][:, 1:3, :])

        def load_q(c):
            nc.sync.dma_start(out=wn[c][:, 0:1, :], in_=w_view[c][:, 0:1, :])

        load_x(0)
        load_kv(0)
        load_x(1)
        load_kv(1)
        load_q(0)
        for c in range(2, NCHUNK):
            load_kv(c)
            load_q(c - 1)
        load_q(NCHUNK - 1)

        ident = const.tile([P, P], F32, name="ident")
        make_identity(nc, ident[:])
        pidx = const.tile([P, 1], I32, name="pidx")
        nc.gpsimd.iota(pidx[:], pattern=[[0, 1]], base=0, channel_multiplier=1)
        ones = const.tile([P, P], F32, name="ones")
        nc.gpsimd.memset(ones[:], 1.0)
        s_i = const.tile([P, 1], I32, name="s_i")
        nc.vector.tensor_single_scalar(out=s_i[:], in_=pidx[:], scalar=15, op=ALU.bitwise_and)
        r_i = const.tile([P, 1], I32, name="r_i")
        nc.vector.tensor_single_scalar(out=r_i[:], in_=pidx[:], scalar=4, op=ALU.logical_shift_right)
        s_f = const.tile([P, 1], F32, name="s_f")
        vcopy(out=s_f[:], in_=s_i[:])
        r_f = const.tile([P, 1], F32, name="r_f")
        vcopy(out=r_f[:], in_=r_i[:])
        tab = const.tile([P, 8], F32, name="tab")
        nc.scalar.activation(out=tab[:, 0:1], in_=s_f[:], func=ACT.Exp, scale=0.125, bias=-1.875)
        nc.scalar.activation(out=tab[:, 1:2], in_=s_f[:], func=ACT.Exp, scale=-0.125)
        for rh in range(2):
            nc.scalar.activation(
                out=tab[:, 2 + rh : 3 + rh], in_=r_f[:], func=ACT.Exp, scale=0.125, bias=(8.0 * rh - 15.0) / 8.0
            )
            nc.scalar.activation(
                out=tab[:, 4 + rh : 5 + rh], in_=r_f[:], func=ACT.Exp, scale=-0.125, bias=-1.0 * rh
            )
        perm = const.tile([P, P], F32, name="perm")
        id_v = ident[:].rearrange("p (bl g u i) -> p g i bl u", bl=2, g=2, u=2, i=16)
        pm_v = perm[:].rearrange("p (g i bl u) -> p g i bl u", g=2, i=16, bl=2, u=2)
        for g in range(2):
            vcopy(out=pm_v[:, g], in_=id_v[:, g])
        b_rows_f = const.tile([P, P], F32, name="b_rows_f")
        nc.vector.memset(b_rows_f[:], 0.0)
        hs = const.tile([P, 1], F32, name="hs")
        nc.vector.scalar_tensor_tensor(
            out=hs[:], in0=tab[:, 0:1], scalar=1.0, in1=tab[:, 1:2], op0=ALU.add, op1=ALU.add
        )
        vcopy(out=b_rows_f[0:24, :], in_=b_rows[:])
        b_ps = bank("tp")
        nc.tensor.transpose(out=b_ps[:, 0, :], in_=b_rows_f[:], identity=ident[:])
        bias = const.tile([P, 24], F32, name="bias")
        vcopy(out=bias[:], in_=b_ps[:, 0, 0:24])
        cb = const.tile([P, NCHUNK], F32, name="cb")
        nc.vector.tensor_mul(out=cb[:], in0=bias[:, 8:16], in1=bias[:, 16:24])
        cbh = const.tile([P, NCHUNK], F32, name="cbh")
        nc.vector.tensor_scalar_mul(out=cbh[:], in0=cb[:], scalar1=hs[:, 0:1])

        xr = [xpool.tile([P, 2048], F32, name="xr%d" % h) for h in range(2)]
        xg = [xpool.tile([P, 4096], BF16, name="xg%d" % g, align_bytes=64) for g in range(2)]
        xc = [xpool.tile([P, NPATCH], U32, name="xc%d" % g, align_bytes=64) for g in range(2)]
        xs = [xpool.tile([P, NPATCH], U8, name="xs%d" % g, align_bytes=64) for g in range(2)]

        def x_reorder(h, q, copy):
            src = xn[h][:].bitcast(F32).rearrange("p (r j s) -> p j r s", r=16, j=16, s=8)
            dst = xr[h][:].rearrange("p (j r s) -> p j r s", j=16, r=16, s=8)
            copy(out=dst[:, 4 * q : 4 * q + 4], in_=src[:, 4 * q : 4 * q + 4])

        def x_bank(h, q, tag, copy):
            t = bank(tag)
            for jj in range(4):
                j = 4 * q + jj
                nc.tensor.transpose(out=t[:, jj, :], in_=xr[h][:, j * P : (j + 1) * P], identity=perm[:])
            src = t[:].rearrange("p j (g i f) -> p j g i f", g=2, i=16, f=4)
            for g in range(2):
                dst = xg[g][:].bitcast(F32).rearrange("p (j i h f) -> p j i h f", j=16, i=16, h=2, f=4)
                copy(out=dst[:, 4 * q : 4 * q + 4, :, h, :], in_=src[:, :, g])

        def x_quant(half, g):
            nc.vector.quantize_mx(
                out=xc[g][:, half * BANK : (half + 1) * BANK].bitcast(FP8X4),
                scales=xs[g][:, half * BANK : (half + 1) * BANK],
                in_=xg[g][:, half * 4 * BANK : (half + 1) * 4 * BANK],
            )

        wg_kv = {}
        wg_q = {}
        wc_kv = {}
        ws_kv = {}
        wc_q = {}
        ws_q = {}

        def w_bank(c, section, dst):
            wt = bank("tp")
            words = wn[c][:, section, :].bitcast(F32)
            for chn in range(4):
                nc.tensor.transpose(out=wt[:, chn, :], in_=words[:, chn * P : (chn + 1) * P], identity=ident[:])
            scopy(out=dst, in_=wt[:].rearrange("p (g u) o -> p g o u", g=2, u=2))

        def w_transpose_kv(c):
            wg_kv[c] = work2.tile([P, 2048], BF16, name="wgkv", tag="wgkv", align_bytes=64)
            v = wg_kv[c][:].bitcast(F32).rearrange("p (t g o u) -> p t g o u", t=2, g=2, o=P, u=2)
            w_bank(c, 1, v[:, 0])
            w_bank(c, 2, v[:, 1])

        def w_transpose_q(c):
            wg_q[c] = work2.tile([P, 1024], BF16, name="wgq", tag="wgq", align_bytes=64)
            w_bank(c, 0, wg_q[c][:].bitcast(F32).rearrange("p (g o u) -> p g o u", g=2, o=P, u=2))

        def w_quant_kv(c):
            wc_kv[c] = work3.tile([P, 512], U32, name="wckv", tag="wckv", align_bytes=64)
            ws_kv[c] = work3.tile([P, 512], U8, name="wskv", tag="wskv", align_bytes=64)
            nc.vector.quantize_mx(out=wc_kv[c][:].bitcast(FP8X4), scales=ws_kv[c][:], in_=wg_kv[c][:])

        def w_quant_q(c):
            wc_q[c] = work3.tile([P, 256], U32, name="wcq", tag="wcq", align_bytes=64)
            ws_q[c] = work3.tile([P, 256], U8, name="wsq", tag="wsq", align_bytes=64)
            nc.vector.quantize_mx(out=wc_q[c][:].bitcast(FP8X4), scales=ws_q[c][:], in_=wg_q[c][:])

        def mx(codes, scales, first, half, tag):
            acc = ps_mx.tile([P, BANK], F32, name="acc", tag=tag)
            pats = slice(half * BANK, (half + 1) * BANK)
            for g in range(2):
                cols = slice(first + g * P, first + (g + 1) * P)
                nc.tensor.matmul_mx(
                    out=acc[:],
                    lhsT=codes[:, cols].bitcast(FP8X4),
                    lhsT_scale=scales[:, cols],
                    rhs=xc[g][:, pats].bitcast(FP8X4),
                    rhs_scale=xs[g][:, pats],
                    start=(g == 0),
                    stop=(g == 1),
                )
            return acc

        ks = {}
        v_ps = {}
        q_ps = {}
        kv = {}
        tt = {}
        pt = {}
        qt = {}
        zt = {}
        ut = {}
        o_tiles = {}
        os_tiles = {}

        def borders(c):
            kv[c] = work2.tile([P, 18, YJ], F32, name="kv", tag="kv")
            nc.scalar.activation(
                out=kv[c][:, 0:18:17, :],
                in_=ones[:].rearrange("p (a y) -> p a y", a=2),
                func=ACT.Copy,
                scale=cb[:, c : c + 1],
            )
            tt[c] = work3.tile([P, 16, TROW], F32, name="tt", tag="tt")
            nc.scalar.activation(
                out=tt[c][:].rearrange("p j (l f) -> p j l f", f=4)[:, :, 1:19:17, :],
                in_=ones[:].rearrange("p (j l f) -> p j l f", j=16, l=2, f=4),
                func=ACT.Copy,
                scale=cbh[:, c : c + 1],
            )

        def front(c, half):
            if half == 0:
                ks[c] = work2.tile([P, NPATCH], F32, name="ks", tag="ks")
            k_ps = mx(wc_kv[c], ws_kv[c], 0, half, "acc0")
            v_ps[(c, half)] = mx(wc_kv[c], ws_kv[c], 256, half, "acc1")
            nc.scalar.activation(
                out=ks[c][:, half * BANK : (half + 1) * BANK], in_=k_ps[:], func=ACT.Identity,
                bias=bias[:, 8 + c : 9 + c], scale=1.0,
            )

        def mx_q(c):
            for half in range(2):
                q_ps[(c, half)] = mx(wc_q[c], ws_q[c], 0, half, "acc2")

        def stt(o, a, s, b, op0, op1):
            nc.vector.scalar_tensor_tensor(out=o, in0=a, scalar=s, in1=b, op0=op0, op1=op1)

        def st_k(c, half):
            flat = kv[c][:].rearrange("p a y -> p (a y)")
            stt(
                flat[:, YJ + half * BANK : YJ + (half + 1) * BANK], v_ps[(c, half)][:], bias[:, 16 + c : 17 + c],
                ks[c][:, half * BANK : (half + 1) * BANK], ALU.add, ALU.mult,
            )

        def st_h1(c):
            flat = kv[c][:].rearrange("p a y -> p (a y)")
            pt[c] = work1.tile([P, 16, YJ], F32, name="pt", tag="pt")
            stt(
                pt[c][:].rearrange("p j y -> p (j y)"), flat[:, 0:NPATCH], tab[:, 0:1], flat[:, YJ : YJ + NPATCH],
                ALU.mult, ALU.add,
            )

        def st_h2(c):
            stt(tt[c][:, :, 8:72], kv[c][:, 2:18, :], tab[:, 1:2], pt[c][:], ALU.mult, ALU.add)

        def st_v1(c):
            rh = c % 2
            qt[c] = work2.tile([P, 16, YJ], F32, name="qt", tag="qt")
            ut[c] = work2.tile([P, 16, YJ], F32, name="ut", tag="ut")
            stt(qt[c][:], tt[c][:, :, 4:68], tab[:, 2 + rh : 3 + rh], tt[c][:, :, 8:72], ALU.mult, ALU.add)

        def st_z(c):
            rh = c % 2
            zt[c] = work2.tile([P, GP_J, YJ], F32, name="zt", tag="zt")
            nc.scalar.activation(
                out=zt[c][:], in_=tt[c][:, 0:GP_J, 12:76], func=ACT.Copy, scale=tab[:, 4 + rh : 5 + rh]
            )

        def st_g(c):
            nc.gpsimd.tensor_tensor(out=ut[c][:, 0:GP_J, :], in0=qt[c][:, 0:GP_J, :], in1=zt[c][:], op=ALU.add)

        def st_v2(c, js):
            rh = c % 2
            stt(ut[c][:, js, :], tt[c][:, js, 12:76], tab[:, 4 + rh : 5 + rh], qt[c][:, js, :], ALU.mult, ALU.add)

        def st_f(c, half):
            ch = c // 2
            rh = c % 2
            if ch not in o_tiles:
                o_tiles[ch] = work2.tile([P, 2048], F32, name="ot", tag="ot")
            o_v = o_tiles[ch][:].rearrange("p (n a b) -> p n a b", a=2, b=4)
            stt(
                o_v[:, half * P : (half + 1) * P, rh, :],
                q_ps[(c, half)][:].rearrange("p (n b) -> p n b", b=4),
                bias[:, c : c + 1],
                ut[c][:].rearrange("p j (i b) -> p (j i) b", b=4)[:, half * P : (half + 1) * P, :],
                ALU.add, ALU.mult,
            )

        def out_bank(ch, q, copy, tag):
            if ch not in os_tiles:
                os_tiles[ch] = work2.tile([P, 8, 16, 16], F32, name="os_t", tag="os")
            tp = bank(tag)
            for jj in range(4):
                j = 4 * q + jj
                nc.tensor.transpose(out=tp[:, jj, :], in_=o_tiles[ch][:, j * P : (j + 1) * P], identity=ident[:])
            copy(
                out=os_tiles[ch][:, :, 4 * q : 4 * q + 4, :],
                in_=tp[:].rearrange("p j (r s) -> p r j s", r=8, s=16),
            )

        def out_store(ch):
            os_flat = os_tiles[ch][:].rearrange("p r j s -> p (r j s)")
            for b in range(4):
                nc.sync.dma_start(
                    out=out[b, ch].rearrange("(m r) w -> m (r w)", r=8), in_=os_flat[b : b + 125 : 4, :]
                )

        borders(0)
        x_reorder(0, 0, vcopy)
        x_reorder(0, 1, scopy)
        x_reorder(0, 2, vcopy)
        x_reorder(0, 3, vcopy)
        x_bank(0, 0, "acc0", vcopy)
        x_bank(0, 1, "acc0", scopy)
        x_bank(0, 2, "acc1", vcopy)
        x_bank(0, 3, "acc1", scopy)
        x_reorder(1, 0, vcopy)
        x_reorder(1, 1, scopy)
        x_reorder(1, 2, vcopy)
        x_reorder(1, 3, vcopy)
        w_transpose_kv(0)
        x_bank(1, 0, "acc2", vcopy)
        x_bank(1, 1, "acc2", scopy)
        w_quant_kv(0)
        x_quant(0, 0)
        x_quant(0, 1)
        x_bank(1, 2, "acc0", scopy)
        x_bank(1, 3, "acc1", scopy)
        w_transpose_kv(1)
        front(0, 0)
        x_quant(1, 0)
        x_quant(1, 1)
        front(0, 1)
        w_quant_kv(1)
        w_transpose_kv(2)
        w_transpose_q(0)

        last = NCHUNK - 1
        for p in range(NCHUNK + 2):
            if p <= last:
                st_k(p, 0)
                st_k(p, 1)
            if 1 <= p <= last and GP_J > 0:
                st_g(p - 1)
            if 2 <= p <= last + 1:
                st_f(p - 2, 0)
                st_f(p - 2, 1)
            if p == last + 2:
                st_f(last, 0)
                out_bank(3, 0, scopy, "tp")
                out_bank(3, 1, scopy, "tp")
                st_f(last, 1)
                out_bank(3, 2, vcopy, "acc0")
                out_bank(3, 3, scopy, "acc1")
                out_store(3)
            if p + 1 <= last:
                borders(p + 1)
                front(p + 1, 0)
                front(p + 1, 1)
            if 1 <= p <= last + 1:
                mx_q(p - 1)
            if p <= last:
                st_h1(p)
            if 1 <= p <= last and GP_J < 16:
                st_v2(p - 1, slice(GP_J, 16))
            if p == last + 1:
                st_v2(last, slice(0, 8))
                st_v2(last, slice(8, 16))
            if p <= last:
                st_h2(p)
            if p < last and GP_J > 0:
                st_z(p)
            if p in (3, 5, 7):
                ch = (p - 3) // 2
                for q in range(4):
                    out_bank(ch, q, scopy, "tp")
                out_store(ch)
            if p + 2 <= last:
                w_quant_kv(p + 2)
            if p <= last:
                w_quant_q(p)
                st_v1(p)
            if p + 3 <= last:
                w_transpose_kv(p + 3)
            if p + 1 <= last:
                w_transpose_q(p + 1)
